import numpy as np
import ml_dtypes


def mxq(x, axis, fmt="e4m3"):
    dtype, down = {"e4m3": (ml_dtypes.float8_e4m3fn, 7), "e5m2": (ml_dtypes.float8_e5m2, 14)}[fmt]
    v = np.moveaxis(np.asarray(x, np.float32).astype(ml_dtypes.bfloat16).astype(np.float64), axis, -1)
    blocks = v.reshape(v.shape[:-1] + (-1, 32))
    amax = np.abs(blocks).max(-1, keepdims=True)
    byte = np.maximum(np.where(amax > 0, np.frexp(amax)[1] - 1 + 127, 0) - down, 1)
    scale = np.exp2(byte - 127.0)
    codes = (blocks / scale).astype(np.float32).astype(dtype).astype(np.float64)
    return np.moveaxis((codes * scale).reshape(v.shape), -1, axis)


WIDE = False


def mx_kscale(k):
    if not WIDE:
        return np.ones(k)
    levels = np.array([10, -10, 5, -5, 0])
    a = np.random.permutation(np.resize(levels, k // 512 * 4)).reshape(k // 512, 4)
    idx = np.arange(k)
    return np.exp2(a[idx // 512, idx % 128 // 32])


BF16 = ml_dtypes.bfloat16


def bf(x):
    return np.asarray(x, np.float32).astype(BF16)


def f64(x):
    return np.asarray(x).astype(np.float64)


E2M1 = np.array([0.0, 0.5, 1.0, 1.5, 2.0, 3.0, 4.0, 6.0, -0.0, -0.5, -1.0, -1.5, -2.0, -3.0, -4.0, -6.0])


def pack_weight(w, fmt):
    k, n = w.shape
    w = f64(bf(w)).reshape(k // 32, 32, n)
    amax = np.abs(w).max(1)
    if fmt == "e4m3":
        byte = np.frexp(amax)[1] - 1 + 127 - 7
    else:
        mant, ex = np.frexp(amax / 6.0)
        byte = np.where(mant > 0.5, ex, ex - 1) + 127
    byte = np.clip(np.where(amax > 0, byte, 1), 1, 254)
    scaled = (w * np.exp2(127.0 - byte)[:, None, :]).reshape(k, n).astype(np.float32)
    by_word = np.ascontiguousarray(scaled.reshape(k // 512, 128, 4, n).transpose(0, 1, 3, 2))
    if fmt == "e4m3":
        words = by_word.astype(ml_dtypes.float8_e4m3fn).view(np.uint8)
    else:
        c = by_word.astype(ml_dtypes.float4_e2m1fn).view(np.uint8) & 0xF
        words = c[..., 0::2] | (c[..., 1::2] << 4)
    return np.ascontiguousarray(words), np.ascontiguousarray(byte.astype(np.uint8).reshape(k // 512, 16, n))


def unpack_weight(words, scales, fmt):
    g, p, n, _ = words.shape
    if fmt == "e4m3":
        vals = np.ascontiguousarray(words).view(ml_dtypes.float8_e4m3fn).astype(np.float64)
    else:
        nib = np.empty((g, p, n, 4), np.uint8)
        nib[..., 0::2] = words & 0xF
        nib[..., 1::2] = words >> 4
        vals = E2M1[nib]
    vals = vals * np.repeat(np.exp2(scales.astype(np.float64) - 127.0), 8, axis=1)[..., None]
    return vals.transpose(0, 1, 3, 2).reshape(g * 512, n)


T, B, D, H, HD, A = 2048, 2, 1024, 1, 128, 128
HH = H * HD
HA = H * A
N = HH + HH + HA + HA
EPS = 1e-5
QK = 1.5


def layer_norm(x, w, b):
    mu = x.mean(-1, keepdims=True)
    var = np.square(x - mu).mean(-1, keepdims=True)
    return (x - mu) * (1.0 / np.sqrt(var + EPS)) * w + b


def setup_inputs():
    s = mx_kscale(D)
    col = np.concatenate([np.ones(HH + HH), QK * np.ones(HA + HA)])
    src = bf(np.random.standard_normal((T, B, D)))
    ln1_w = bf((1.0 + 0.1 * np.random.standard_normal(D)) * s)
    ln1_b = bf(0.1 * np.random.standard_normal(D) * s)
    words, scales = pack_weight(np.random.standard_normal((D, N)) * col / np.sqrt(D) / s[:, None], "e4m3")
    b_uvqk = bf(0.1 * np.random.standard_normal(N))
    return {"src": src,
            "ln1_w": ln1_w,
            "ln1_b": ln1_b,
            "w_uvqk_words": words,
            "w_uvqk_scales": scales,
            "b_uvqk": b_uvqk}


def reference(src, ln1_w, ln1_b, w_uvqk_words, w_uvqk_scales, b_uvqk):
    src_norm = layer_norm(f64(src), f64(ln1_w), f64(ln1_b))
    return (mxq(src_norm, 2, "e4m3") @ unpack_weight(w_uvqk_words, w_uvqk_scales, "e4m3")) + f64(b_uvqk)

@@ -1,0 +1,171 @@
+from contextlib import ExitStack
+
+import concourse.mybir as mybir
+from concourse.masks import make_identity
+
+FP8X4 = mybir.dt.float8_e4m3fn_x4
+BF16 = mybir.dt.bfloat16
+F32 = mybir.dt.float32
+I32 = mybir.dt.int32
+U32 = mybir.dt.uint32
+U8 = mybir.dt.uint8
+ALU = mybir.AluOpType
+ACT = mybir.ActivationFunctionType
+
+P = 128
+PACK = 4
+K_PASS = P * PACK
+ROWS = 2048 * 2
+D = 1024
+N = 512
+PASSES = D // K_PASS
+PLANES = PASSES * PACK
+TILES = 4
+GROUP_ROWS = TILES * P
+GROUPS = ROWS // GROUP_ROWS
+BN_CHUNK = 512
+BN_CHUNKS = D // BN_CHUNK
+BN_STATS_DIM = 6
+BN_AGGR_DIM = 2
+EPS = 1e-5
+
+FLOPS = 2 * ROWS * D * N
+
+
+def tile_stulayer_pa_t_kernel(tc, src, ln1_w, ln1_b, w_uvqk_words, w_uvqk_scales, b_uvqk, out):
+    nc = tc.nc
+    src_groups = src.rearrange("t b d -> (t b) d").rearrange("(s p j) d -> s p j d", p=P, j=TILES)
+    out_groups = out.rearrange("t b n -> (t b) n").rearrange("(s p j) n -> s p j n", p=P, j=TILES)
+
+    with ExitStack() as ctx:
+        consts = ctx.enter_context(tc.tile_pool(name="consts", bufs=1))
+        x_pool = ctx.enter_context(tc.tile_pool(name="x", bufs=GROUPS))
+        small = ctx.enter_context(tc.tile_pool(name="small", bufs=4))
+        xhat_pool = ctx.enter_context(tc.tile_pool(name="xhat", bufs=3))
+        plane_pool = ctx.enter_context(tc.tile_pool(name="planes", bufs=3))
+        mx_pool = ctx.enter_context(tc.tile_pool(name="mx", bufs=3))
+        out_pool = ctx.enter_context(tc.tile_pool(name="outs", bufs=3))
+        psum_t = ctx.enter_context(tc.psum_pool(name="psum_t", bufs=4))
+        psum_acc = ctx.enter_context(tc.psum_pool(name="psum_acc", bufs=4))
+
+        w_scales = consts.tile([P, PASSES, N], U8, align_bytes=64)
+        nc.vector.memset(w_scales[:].rearrange("p g n -> p (g n)").bitcast(I32), 0)
+        x_tiles = []
+        x_first = x_pool.tile([P, TILES, D], BF16, name="x_sb")
+        nc.sync.dma_start(out=x_first[:], in_=src_groups[0])
+        x_tiles.append(x_first)
+        for g in range(PASSES):
+            for quadrant in range(4):
+                nc.sync.dma_start(
+                    out=w_scales[32 * quadrant : 32 * quadrant + 4, g, :].bitcast(I32),
+                    in_=w_uvqk_scales[g, 4 * quadrant : 4 * quadrant + 4, :].bitcast(I32),
+                )
+        w_words = consts.tile([P, PASSES, N], U32, align_bytes=64)
+        for g in range(PASSES):
+            nc.sync.dma_start(
+                out=w_words[:, g, :].bitcast(I32),
+                in_=w_uvqk_words[g].rearrange("p n t -> p (n t)").bitcast(I32),
+            )
+
+        gain_bf = consts.tile([P, PASSES, PACK], BF16)
+        shift_bf = consts.tile([P, PASSES, PACK], BF16)
+        with nc.allow_non_contiguous_dma(reason="2 KiB vectors in runs of four features"):
+            nc.scalar.dma_start(out=gain_bf[:], in_=ln1_w.rearrange("(g p t) -> p g t", p=P, t=PACK))
+            nc.scalar.dma_start(out=shift_bf[:], in_=ln1_b.rearrange("(g p t) -> p g t", p=P, t=PACK))
+        gain = consts.tile([P, PLANES], F32)
+        shift = consts.tile([P, PLANES], F32)
+        nc.vector.tensor_copy(out=gain[:], in_=gain_bf[:].rearrange("p g t -> p (g t)"))
+        nc.vector.tensor_copy(out=shift[:], in_=shift_bf[:].rearrange("p g t -> p (g t)"))
+        bias_bf = consts.tile([P, N], BF16)
+        nc.scalar.dma_start(out=bias_bf[:], in_=b_uvqk.partition_broadcast(P))
+        bias = consts.tile([P, N], F32)
+        nc.vector.tensor_copy(out=bias[:], in_=bias_bf[:])
+        eps = consts.tile([P, 1], F32)
+        nc.vector.memset(eps[:], EPS)
+        identity = consts.tile([P, P], F32)
+        make_identity(nc, identity[:])
+
+        for s in range(1, GROUPS):
+            x_sb = x_pool.tile([P, TILES, D], BF16, name="x_sb")
+            nc.sync.dma_start(out=x_sb[:], in_=src_groups[s])
+            x_tiles.append(x_sb)
+
+        for s in range(GROUPS):
+            x_sb = x_tiles[s]
+
+            stats = small.tile([P, TILES, BN_CHUNKS, BN_STATS_DIM], F32)
+            mean_var = small.tile([P, TILES, BN_AGGR_DIM], F32)
+            for j in range(TILES):
+                for c in range(BN_CHUNKS):
+                    nc.vector.bn_stats(out=stats[:, j, c, :], in_=x_sb[:, j, c * BN_CHUNK : (c + 1) * BN_CHUNK])
+                nc.vector.bn_aggr(out=mean_var[:, j, :], in_=stats[:, j].rearrange("p c v -> p (c v)"))
+            std = small.tile([P, TILES], F32)
+            nc.scalar.activation(out=std[:], in_=mean_var[:, :, 1], func=ACT.Sqrt, bias=eps[:], scale=1.0)
+            rstd = small.tile([P, TILES], F32)
+            nc.vector.reciprocal(out=rstd[:], in_=std[:])
+            neg_mean = small.tile([P, TILES], F32)
+            nc.vector.tensor_scalar_mul(out=neg_mean[:], in0=mean_var[:, :, 0], scalar1=-1.0)
+
+            xhat = xhat_pool.tile([P, TILES, PLANES, P], F32)
+            for g in range(PASSES):
+                for j in range(TILES):
+                    nc.gpsimd.tensor_scalar(
+                        out=xhat[:, j, g * PACK : (g + 1) * PACK, :],
+                        in0=x_sb[:, j, g * K_PASS : (g + 1) * K_PASS].rearrange("p (q t) -> p t q", t=PACK),
+                        scalar1=neg_mean[:, j : j + 1],
+                        scalar2=rstd[:, j : j + 1],
+                        op0=ALU.add,
+                        op1=ALU.mult,
+                    )
+
+            planes = plane_pool.tile([P, PLANES, GROUP_ROWS], BF16)
+            for plane in range(PLANES):
+                xt = psum_t.tile([P, GROUP_ROWS], F32)
+                for j in range(TILES):
+                    nc.tensor.transpose(xt[:, j * P : (j + 1) * P], xhat[:, j, plane, :], identity[:])
+                nc.scalar.activation(
+                    out=planes[:, plane, :],
+                    in_=xt[:],
+                    func=ACT.Identity,
+                    scale=gain[:, plane : plane + 1],
+                    bias=shift[:, plane : plane + 1],
+                )
+
+            grouped = mx_pool.tile([P, PASSES, GROUP_ROWS, PACK], BF16, align_bytes=64)
+            codes = mx_pool.tile([P, PASSES, GROUP_ROWS], U32, align_bytes=64)
+            scales = mx_pool.tile([P, PASSES, GROUP_ROWS], U8, align_bytes=64)
+            nc.scalar.copy(
+                out=grouped[:, 0].rearrange("p (c i) t -> p c t i", i=4),
+                in_=planes[:, 0:PACK, :].rearrange("p t (c i) -> p c t i", i=4),
+            )
+            nc.gpsimd.tensor_scalar(
+                out=grouped[:, 1],
+                in0=planes[:, PACK : 2 * PACK, :].rearrange("p t r -> p r t"),
+                scalar1=1.0,
+                scalar2=0.0,
+                op0=ALU.mult,
+                op1=ALU.add,
+            )
+            for g in range(PASSES):
+                nc.vector.quantize_mx(
+                    out=codes[:, g, :].bitcast(FP8X4),
+                    scales=scales[:, g, :],
+                    in_=grouped[:, g].rearrange("p r t -> p (r t)"),
+                )
+
+            out_sb = out_pool.tile([P, TILES, N], F32)
+            for j in range(TILES):
+                rows = slice(j * P, (j + 1) * P)
+                acc = psum_acc.tile([P, N], F32)
+                for g in range(PASSES):
+                    nc.tensor.matmul_mx(
+                        out=acc[:],
+                        lhsT=codes[:, g, rows].bitcast(FP8X4),
+                        lhsT_scale=scales[:, g, rows],
+                        rhs=w_words[:, g, :].bitcast(FP8X4),
+                        rhs_scale=w_scales[:, g, :],
+                        start=(g == 0),
+                        stop=(g == PASSES - 1),
+                    )
+                nc.vector.tensor_tensor(out=out_sb[:, j, :], in0=acc[:], in1=bias[:], op=ALU.add)
+            nc.sync.dma_start(out=out_groups[s], in_=out_sb[:])

@@ -103,20 +103,17 @@ def tile_stulayer_pa_t_kernel(tc, src, ln1_w, ln1_b, w_uvqk_words, w_uvqk_scales
             nc.scalar.activation(out=std[:], in_=mean_var[:, :, 1], func=ACT.Sqrt, bias=eps[:], scale=1.0)
             rstd = small.tile([P, TILES], F32)
             nc.vector.reciprocal(out=rstd[:], in_=std[:])
-            neg_mean = small.tile([P, TILES], F32)
-            nc.vector.tensor_scalar_mul(out=neg_mean[:], in0=mean_var[:, :, 0], scalar1=-1.0)
 
             xhat = xhat_pool.tile([P, TILES, PLANES, P], F32)
-            for g in range(PASSES):
-                for j in range(TILES):
-                    nc.gpsimd.tensor_scalar(
-                        out=xhat[:, j, g * PACK : (g + 1) * PACK, :],
-                        in0=x_sb[:, j, g * K_PASS : (g + 1) * K_PASS].rearrange("p (q t) -> p t q", t=PACK),
-                        scalar1=neg_mean[:, j : j + 1],
-                        scalar2=rstd[:, j : j + 1],
-                        op0=ALU.add,
-                        op1=ALU.mult,
-                    )
+            for j in range(TILES):
+                nc.vector.tensor_scalar(
+                    out=xhat[:, j].rearrange("p (g t) q -> p g t q", t=PACK),
+                    in0=x_sb[:, j, :].rearrange("p (g q t) -> p g t q", q=P, t=PACK),
+                    scalar1=mean_var[:, j, 0:1],
+                    scalar2=rstd[:, j : j + 1],
+                    op0=ALU.subtract,
+                    op1=ALU.mult,
+                )
 
             planes = plane_pool.tile([P, PLANES, GROUP_ROWS], BF16)
             for plane in range(PLANES):
@@ -134,18 +131,11 @@ def tile_stulayer_pa_t_kernel(tc, src, ln1_w, ln1_b, w_uvqk_words, w_uvqk_scales
             grouped = mx_pool.tile([P, PASSES, GROUP_ROWS, PACK], BF16, align_bytes=64)
             codes = mx_pool.tile([P, PASSES, GROUP_ROWS], U32, align_bytes=64)
             scales = mx_pool.tile([P, PASSES, GROUP_ROWS], U8, align_bytes=64)
-            nc.scalar.copy(
-                out=grouped[:, 0].rearrange("p (c i) t -> p c t i", i=4),
-                in_=planes[:, 0:PACK, :].rearrange("p t (c i) -> p c t i", i=4),
-            )
-            nc.gpsimd.tensor_scalar(
-                out=grouped[:, 1],
-                in0=planes[:, PACK : 2 * PACK, :].rearrange("p t r -> p r t"),
-                scalar1=1.0,
-                scalar2=0.0,
-                op0=ALU.mult,
-                op1=ALU.add,
-            )
+            for g in range(PASSES):
+                nc.scalar.copy(
+                    out=grouped[:, g].rearrange("p (c i) t -> p c t i", i=4),
+                    in_=planes[:, g * PACK : (g + 1) * PACK, :].rearrange("p t (c i) -> p c t i", i=4),
+                )
             for g in range(PASSES):
                 nc.vector.quantize_mx(
                     out=codes[:, g, :].bitcast(FP8X4),

@@ -103,15 +103,17 @@ def tile_stulayer_pa_t_kernel(tc, src, ln1_w, ln1_b, w_uvqk_words, w_uvqk_scales
             nc.scalar.activation(out=std[:], in_=mean_var[:, :, 1], func=ACT.Sqrt, bias=eps[:], scale=1.0)
             rstd = small.tile([P, TILES], F32)
             nc.vector.reciprocal(out=rstd[:], in_=std[:])
+            neg_mean = small.tile([P, TILES], F32)
+            nc.vector.tensor_scalar_mul(out=neg_mean[:], in0=mean_var[:, :, 0], scalar1=-1.0)
 
             xhat = xhat_pool.tile([P, TILES, PLANES, P], F32)
             for j in range(TILES):
-                nc.vector.tensor_scalar(
+                nc.gpsimd.tensor_scalar(
                     out=xhat[:, j].rearrange("p (g t) q -> p g t q", t=PACK),
                     in0=x_sb[:, j, :].rearrange("p (g q t) -> p g t q", q=P, t=PACK),
-                    scalar1=mean_var[:, j, 0:1],
+                    scalar1=neg_mean[:, j : j + 1],
                     scalar2=rstd[:, j : j + 1],
-                    op0=ALU.subtract,
+                    op0=ALU.add,
                     op1=ALU.mult,
                 )
 
@@ -131,11 +133,14 @@ def tile_stulayer_pa_t_kernel(tc, src, ln1_w, ln1_b, w_uvqk_words, w_uvqk_scales
             grouped = mx_pool.tile([P, PASSES, GROUP_ROWS, PACK], BF16, align_bytes=64)
             codes = mx_pool.tile([P, PASSES, GROUP_ROWS], U32, align_bytes=64)
             scales = mx_pool.tile([P, PASSES, GROUP_ROWS], U8, align_bytes=64)
-            for g in range(PASSES):
-                nc.scalar.copy(
-                    out=grouped[:, g].rearrange("p (c i) t -> p c t i", i=4),
-                    in_=planes[:, g * PACK : (g + 1) * PACK, :].rearrange("p t (c i) -> p c t i", i=4),
-                )
+            nc.scalar.copy(
+                out=grouped[:, 0].rearrange("p (c i) t -> p c t i", i=4),
+                in_=planes[:, 0:PACK, :].rearrange("p t (c i) -> p c t i", i=4),
+            )
+            nc.vector.tensor_copy(
+                out=grouped[:, 1].rearrange("p (c i) t -> p c t i", i=4),
+                in_=planes[:, PACK : 2 * PACK, :].rearrange("p t (c i) -> p c t i", i=4),
+            )
             for g in range(PASSES):
                 nc.vector.quantize_mx(
                     out=codes[:, g, :].bitcast(FP8X4),

@@ -32,6 +32,11 @@ EPS = 1e-5
 FLOPS = 2 * ROWS * D * N
 
 
+LAG = 2
+HALVES = 2
+HALF = TILES // HALVES
+
+
 def tile_stulayer_pa_t_kernel(tc, src, ln1_w, ln1_b, w_uvqk_words, w_uvqk_scales, b_uvqk, out):
     nc = tc.nc
     src_groups = src.rearrange("t b d -> (t b) d").rearrange("(s p j) d -> s p j d", p=P, j=TILES)
@@ -43,17 +48,27 @@ def tile_stulayer_pa_t_kernel(tc, src, ln1_w, ln1_b, w_uvqk_words, w_uvqk_scales
         small = ctx.enter_context(tc.tile_pool(name="small", bufs=4))
         xhat_pool = ctx.enter_context(tc.tile_pool(name="xhat", bufs=3))
         plane_pool = ctx.enter_context(tc.tile_pool(name="planes", bufs=3))
-        mx_pool = ctx.enter_context(tc.tile_pool(name="mx", bufs=3))
+        grouped_pool = ctx.enter_context(tc.tile_pool(name="grouped", bufs=PASSES * (LAG + 1)))
+        mx_pool = ctx.enter_context(tc.tile_pool(name="mx", bufs=2))
         out_pool = ctx.enter_context(tc.tile_pool(name="outs", bufs=3))
         psum_t = ctx.enter_context(tc.psum_pool(name="psum_t", bufs=4))
-        psum_acc = ctx.enter_context(tc.psum_pool(name="psum_acc", bufs=4))
+        psum_acc = ctx.enter_context(tc.psum_pool(name="psum_acc", bufs=TILES))
+        ctx.enter_context(tc.manual_schedule())
 
         w_scales = consts.tile([P, PASSES, N], U8, align_bytes=64)
         nc.vector.memset(w_scales[:].rearrange("p g n -> p (g n)").bitcast(I32), 0)
         x_tiles = []
-        x_first = x_pool.tile([P, TILES, D], BF16, name="x_sb")
-        nc.sync.dma_start(out=x_first[:], in_=src_groups[0])
-        x_tiles.append(x_first)
+        for s in range(GROUPS):
+            x_sb = x_pool.tile([P, TILES, D], BF16, name="x_sb")
+            x_tiles.append(x_sb)
+
+        def load(s):
+            for h in range(HALVES):
+                tiles = slice(h * HALF, (h + 1) * HALF)
+                nc.sync.dma_start(out=x_tiles[s][:, tiles, :], in_=src_groups[s][:, tiles, :])
+
+        load(0)
+        load(1)
         for g in range(PASSES):
             for quadrant in range(4):
                 nc.sync.dma_start(
@@ -66,95 +81,117 @@ def tile_stulayer_pa_t_kernel(tc, src, ln1_w, ln1_b, w_uvqk_words, w_uvqk_scales
                 out=w_words[:, g, :].bitcast(I32),
                 in_=w_uvqk_words[g].rearrange("p n t -> p (n t)").bitcast(I32),
             )
+        for s in range(2, GROUPS):
+            load(s)
 
         gain_bf = consts.tile([P, PASSES, PACK], BF16)
         shift_bf = consts.tile([P, PASSES, PACK], BF16)
         with nc.allow_non_contiguous_dma(reason="2 KiB vectors in runs of four features"):
             nc.scalar.dma_start(out=gain_bf[:], in_=ln1_w.rearrange("(g p t) -> p g t", p=P, t=PACK))
             nc.scalar.dma_start(out=shift_bf[:], in_=ln1_b.rearrange("(g p t) -> p g t", p=P, t=PACK))
-        gain = consts.tile([P, PLANES], F32)
-        shift = consts.tile([P, PLANES], F32)
-        nc.vector.tensor_copy(out=gain[:], in_=gain_bf[:].rearrange("p g t -> p (g t)"))
-        nc.vector.tensor_copy(out=shift[:], in_=shift_bf[:].rearrange("p g t -> p (g t)"))
         bias_bf = consts.tile([P, N], BF16)
         nc.scalar.dma_start(out=bias_bf[:], in_=b_uvqk.partition_broadcast(P))
-        bias = consts.tile([P, N], F32)
-        nc.vector.tensor_copy(out=bias[:], in_=bias_bf[:])
-        eps = consts.tile([P, 1], F32)
-        nc.vector.memset(eps[:], EPS)
+
         identity = consts.tile([P, P], F32)
         make_identity(nc, identity[:])
+        eps = consts.tile([P, 1], F32)
+        nc.vector.memset(eps[:], EPS)
+        warm = consts.tile([P, 1], F32)
+        nc.scalar.activation(out=warm[:], in_=eps[:], func=ACT.Sqrt)
 
-        for s in range(1, GROUPS):
-            x_sb = x_pool.tile([P, TILES, D], BF16, name="x_sb")
-            nc.sync.dma_start(out=x_sb[:], in_=src_groups[s])
-            x_tiles.append(x_sb)
+        chunk_stats = {}
+        mean_vars = {}
+        stds = {}
+        rstds = {}
+        xhats = {}
+        groupeds = {}
+        operands = {}
+        accs = {}
 
-        for s in range(GROUPS):
-            x_sb = x_tiles[s]
-
-            stats = small.tile([P, TILES, BN_CHUNKS, BN_STATS_DIM], F32)
-            mean_var = small.tile([P, TILES, BN_AGGR_DIM], F32)
+        def chunk_statistics(s):
+            stats = small.tile([P, TILES, BN_CHUNKS, BN_STATS_DIM], F32, name="stats")
             for j in range(TILES):
                 for c in range(BN_CHUNKS):
-                    nc.vector.bn_stats(out=stats[:, j, c, :], in_=x_sb[:, j, c * BN_CHUNK : (c + 1) * BN_CHUNK])
-                nc.vector.bn_aggr(out=mean_var[:, j, :], in_=stats[:, j].rearrange("p c v -> p (c v)"))
-            std = small.tile([P, TILES], F32)
-            nc.scalar.activation(out=std[:], in_=mean_var[:, :, 1], func=ACT.Sqrt, bias=eps[:], scale=1.0)
-            rstd = small.tile([P, TILES], F32)
-            nc.vector.reciprocal(out=rstd[:], in_=std[:])
-            neg_mean = small.tile([P, TILES], F32)
-            nc.vector.tensor_scalar_mul(out=neg_mean[:], in0=mean_var[:, :, 0], scalar1=-1.0)
+                    nc.vector.bn_stats(
+                        out=stats[:, j, c, :], in_=x_tiles[s][:, j, c * BN_CHUNK : (c + 1) * BN_CHUNK]
+                    )
+            chunk_stats[s] = stats
 
-            xhat = xhat_pool.tile([P, TILES, PLANES, P], F32)
+        def mean_and_variance(s):
+            mean_var = small.tile([P, TILES, BN_AGGR_DIM], F32, name="mean_var")
             for j in range(TILES):
-                nc.gpsimd.tensor_scalar(
+                nc.vector.bn_aggr(out=mean_var[:, j, :], in_=chunk_stats[s][:, j].rearrange("p c v -> p (c v)"))
+            mean_vars[s] = mean_var
+
+        def root(s):
+            std = small.tile([P, TILES], F32, name="std")
+            nc.scalar.activation(out=std[:], in_=mean_vars[s][:, :, 1], func=ACT.Sqrt, bias=eps[:], scale=1.0)
+            stds[s] = std
+
+        def invert_root(s):
+            rstd = small.tile([P, TILES], F32, name="rstd")
+            nc.vector.reciprocal(out=rstd[:], in_=stds[s][:])
+            rstds[s] = rstd
+
+        def normalise(s):
+            xhat = xhat_pool.tile([P, TILES, PLANES, P], F32, name="xhat")
+            for j in range(TILES):
+                nc.vector.tensor_scalar(
                     out=xhat[:, j].rearrange("p (g t) q -> p g t q", t=PACK),
-                    in0=x_sb[:, j, :].rearrange("p (g q t) -> p g t q", q=P, t=PACK),
-                    scalar1=neg_mean[:, j : j + 1],
-                    scalar2=rstd[:, j : j + 1],
-                    op0=ALU.add,
+                    in0=x_tiles[s][:, j, :].rearrange("p (g q t) -> p g t q", q=P, t=PACK),
+                    scalar1=mean_vars[s][:, j, 0:1],
+                    scalar2=rstds[s][:, j : j + 1],
+                    op0=ALU.subtract,
                     op1=ALU.mult,
                 )
+            xhats[s] = xhat
 
-            planes = plane_pool.tile([P, PLANES, GROUP_ROWS], BF16)
-            for plane in range(PLANES):
-                xt = psum_t.tile([P, GROUP_ROWS], F32)
+        def transpose_and_scale(s, g):
+            planes = plane_pool.tile([P, PACK, GROUP_ROWS], BF16, name="planes")
+            for t in range(PACK):
+                plane = g * PACK + t
+                xt = psum_t.tile([P, GROUP_ROWS], F32, name="xt")
                 for j in range(TILES):
-                    nc.tensor.transpose(xt[:, j * P : (j + 1) * P], xhat[:, j, plane, :], identity[:])
+                    nc.tensor.transpose(xt[:, j * P : (j + 1) * P], xhats[s][:, j, plane, :], identity[:])
                 nc.scalar.activation(
-                    out=planes[:, plane, :],
+                    out=planes[:, t, :],
                     in_=xt[:],
                     func=ACT.Identity,
                     scale=gain[:, plane : plane + 1],
                     bias=shift[:, plane : plane + 1],
                 )
+            return planes
 
-            grouped = mx_pool.tile([P, PASSES, GROUP_ROWS, PACK], BF16, align_bytes=64)
-            codes = mx_pool.tile([P, PASSES, GROUP_ROWS], U32, align_bytes=64)
-            scales = mx_pool.tile([P, PASSES, GROUP_ROWS], U8, align_bytes=64)
+        def regroup(s, g, planes):
+            grouped = grouped_pool.tile([P, GROUP_ROWS, PACK], BF16, align_bytes=64, name="grouped")
             nc.scalar.copy(
-                out=grouped[:, 0].rearrange("p (c i) t -> p c t i", i=4),
-                in_=planes[:, 0:PACK, :].rearrange("p t (c i) -> p c t i", i=4),
+                out=grouped[:].rearrange("p (c i) t -> p c t i", i=4),
+                in_=planes[:].rearrange("p t (c i) -> p c t i", i=4),
             )
-            nc.vector.tensor_copy(
-                out=grouped[:, 1].rearrange("p (c i) t -> p c t i", i=4),
-                in_=planes[:, PACK : 2 * PACK, :].rearrange("p t (c i) -> p c t i", i=4),
-            )
+            groupeds[s, g] = grouped
+
+        def quantise(s):
+            codes = mx_pool.tile([P, PASSES, GROUP_ROWS], U32, align_bytes=64, name="codes")
+            scales = mx_pool.tile([P, PASSES, GROUP_ROWS], U8, align_bytes=64, name="scales")
             for g in range(PASSES):
                 nc.vector.quantize_mx(
                     out=codes[:, g, :].bitcast(FP8X4),
                     scales=scales[:, g, :],
-                    in_=grouped[:, g].rearrange("p r t -> p (r t)"),
+                    in_=groupeds[s, g][:].rearrange("p r t -> p (r t)"),
                 )
+            operands[s] = (codes, scales)
 
-            out_sb = out_pool.tile([P, TILES, N], F32)
+        def project(s):
+            codes, scales = operands[s]
+            accs[s] = []
             for j in range(TILES):
-                rows = slice(j * P, (j + 1) * P)
-                acc = psum_acc.tile([P, N], F32)
-                for g in range(PASSES):
+                acc = psum_acc.tile([P, N], F32, name="acc")
+                accs[s].append(acc)
+            for g in range(PASSES):
+                for j in range(TILES):
+                    rows = slice(j * P, (j + 1) * P)
                     nc.tensor.matmul_mx(
-                        out=acc[:],
+                        out=accs[s][j][:],
                         lhsT=codes[:, g, rows].bitcast(FP8X4),
                         lhsT_scale=scales[:, g, rows],
                         rhs=w_words[:, g, :].bitcast(FP8X4),
@@ -162,5 +199,49 @@ def tile_stulayer_pa_t_kernel(tc, src, ln1_w, ln1_b, w_uvqk_words, w_uvqk_scales
                         start=(g == 0),
                         stop=(g == PASSES - 1),
                     )
-                nc.vector.tensor_tensor(out=out_sb[:, j, :], in0=acc[:], in1=bias[:], op=ALU.add)
-            nc.sync.dma_start(out=out_groups[s], in_=out_sb[:])
+
+        def add_bias_and_store(s):
+            out_sb = out_pool.tile([P, TILES, N], F32, name="out_sb")
+            for h in range(HALVES):
+                tiles = slice(h * HALF, (h + 1) * HALF)
+                for j in range(h * HALF, (h + 1) * HALF):
+                    nc.vector.tensor_tensor(out=out_sb[:, j, :], in0=accs[s][j][:], in1=bias[:], op=ALU.add)
+                nc.sync.dma_start(out=out_groups[s][:, tiles, :], in_=out_sb[:, tiles, :])
+
+        gain = consts.tile([P, PLANES], F32)
+        shift = consts.tile([P, PLANES], F32)
+        bias = consts.tile([P, N], F32)
+        chunk_statistics(0)
+        nc.vector.tensor_copy(out=gain[:], in_=gain_bf[:].rearrange("p g t -> p (g t)"))
+        nc.vector.tensor_copy(out=shift[:], in_=shift_bf[:].rearrange("p g t -> p (g t)"))
+        mean_and_variance(0)
+        root(0)
+        nc.vector.tensor_copy(out=bias[:], in_=bias_bf[:])
+        invert_root(0)
+        normalise(0)
+        chunk_statistics(1)
+        mean_and_variance(1)
+
+        for s in range(GROUPS + LAG):
+            if s >= LAG:
+                quantise(s - LAG)
+            if s < GROUPS:
+                planes = transpose_and_scale(s, 0)
+            if s + 1 < GROUPS:
+                root(s + 1)
+            if s >= LAG:
+                project(s - LAG)
+            if s < GROUPS:
+                regroup(s, 0, planes)
+                planes = transpose_and_scale(s, 1)
+                regroup(s, 1, planes)
+            if s + 2 < GROUPS:
+                chunk_statistics(s + 2)
+            if s + 1 < GROUPS:
+                invert_root(s + 1)
+            if s + 2 < GROUPS:
+                mean_and_variance(s + 2)
+            if s + 1 < GROUPS:
+                normalise(s + 1)
+            if s >= LAG:
+                add_bias_and_store(s - LAG)

@@ -35,6 +35,8 @@ FLOPS = 2 * ROWS * D * N
 LAG = 2
 HALVES = 2
 HALF = TILES // HALVES
+PIECES = 4
+PIECE_ROWS = GROUP_ROWS // PIECES
 
 
 def tile_stulayer_pa_t_kernel(tc, src, ln1_w, ln1_b, w_uvqk_words, w_uvqk_scales, b_uvqk, out):
@@ -45,7 +47,7 @@ def tile_stulayer_pa_t_kernel(tc, src, ln1_w, ln1_b, w_uvqk_words, w_uvqk_scales
     with ExitStack() as ctx:
         consts = ctx.enter_context(tc.tile_pool(name="consts", bufs=1))
         x_pool = ctx.enter_context(tc.tile_pool(name="x", bufs=GROUPS))
-        small = ctx.enter_context(tc.tile_pool(name="small", bufs=4))
+        small = ctx.enter_context(tc.tile_pool(name="small", bufs=5))
         xhat_pool = ctx.enter_context(tc.tile_pool(name="xhat", bufs=3))
         plane_pool = ctx.enter_context(tc.tile_pool(name="planes", bufs=3))
         grouped_pool = ctx.enter_context(tc.tile_pool(name="grouped", bufs=PASSES * (LAG + 1)))
@@ -103,19 +105,21 @@ def tile_stulayer_pa_t_kernel(tc, src, ln1_w, ln1_b, w_uvqk_words, w_uvqk_scales
         mean_vars = {}
         stds = {}
         rstds = {}
+        offsets = {}
         xhats = {}
         groupeds = {}
         operands = {}
         accs = {}
 
-        def chunk_statistics(s):
-            stats = small.tile([P, TILES, BN_CHUNKS, BN_STATS_DIM], F32, name="stats")
-            for j in range(TILES):
-                for c in range(BN_CHUNKS):
-                    nc.vector.bn_stats(
-                        out=stats[:, j, c, :], in_=x_tiles[s][:, j, c * BN_CHUNK : (c + 1) * BN_CHUNK]
-                    )
-            chunk_stats[s] = stats
+        def chunk_statistics(s, chunks):
+            if s not in chunk_stats:
+                stats = small.tile([P, TILES, BN_CHUNKS, BN_STATS_DIM], F32, name="stats")
+                chunk_stats[s] = stats
+            for i in chunks:
+                j, c = divmod(i, BN_CHUNKS)
+                nc.vector.bn_stats(
+                    out=chunk_stats[s][:, j, c, :], in_=x_tiles[s][:, j, c * BN_CHUNK : (c + 1) * BN_CHUNK]
+                )
 
         def mean_and_variance(s):
             mean_var = small.tile([P, TILES, BN_AGGR_DIM], F32, name="mean_var")
@@ -133,16 +137,22 @@ def tile_stulayer_pa_t_kernel(tc, src, ln1_w, ln1_b, w_uvqk_words, w_uvqk_scales
             nc.vector.reciprocal(out=rstd[:], in_=stds[s][:])
             rstds[s] = rstd
 
+        def offset(s):
+            off = small.tile([P, TILES], F32, name="off")
+            nc.vector.scalar_tensor_tensor(
+                out=off[:], in0=mean_vars[s][:, :, 0], scalar=-1.0, in1=rstds[s][:], op0=ALU.mult, op1=ALU.mult
+            )
+            offsets[s] = off
+
         def normalise(s):
             xhat = xhat_pool.tile([P, TILES, PLANES, P], F32, name="xhat")
             for j in range(TILES):
-                nc.vector.tensor_scalar(
+                nc.scalar.activation(
                     out=xhat[:, j].rearrange("p (g t) q -> p g t q", t=PACK),
-                    in0=x_tiles[s][:, j, :].rearrange("p (g q t) -> p g t q", q=P, t=PACK),
-                    scalar1=mean_vars[s][:, j, 0:1],
-                    scalar2=rstds[s][:, j : j + 1],
-                    op0=ALU.subtract,
-                    op1=ALU.mult,
+                    in_=x_tiles[s][:, j, :].rearrange("p (g q t) -> p g t q", q=P, t=PACK),
+                    func=ACT.Identity,
+                    scale=rstds[s][:, j : j + 1],
+                    bias=offsets[s][:, j : j + 1],
                 )
             xhats[s] = xhat
 
@@ -164,10 +174,16 @@ def tile_stulayer_pa_t_kernel(tc, src, ln1_w, ln1_b, w_uvqk_words, w_uvqk_scales
 
         def regroup(s, g, planes):
             grouped = grouped_pool.tile([P, GROUP_ROWS, PACK], BF16, align_bytes=64, name="grouped")
-            nc.scalar.copy(
-                out=grouped[:].rearrange("p (c i) t -> p c t i", i=4),
-                in_=planes[:].rearrange("p t (c i) -> p c t i", i=4),
-            )
+            for i in range(PIECES):
+                rows = slice(i * PIECE_ROWS, (i + 1) * PIECE_ROWS)
+                nc.gpsimd.tensor_scalar(
+                    out=grouped[:, rows, :],
+                    in0=planes[:, :, rows].rearrange("p t r -> p r t"),
+                    scalar1=1.0,
+                    scalar2=0.0,
+                    op0=ALU.mult,
+                    op1=ALU.add,
+                )
             groupeds[s, g] = grouped
 
         def quantise(s):
@@ -200,48 +216,59 @@ def tile_stulayer_pa_t_kernel(tc, src, ln1_w, ln1_b, w_uvqk_words, w_uvqk_scales
                         stop=(g == PASSES - 1),
                     )
 
-        def add_bias_and_store(s):
-            out_sb = out_pool.tile([P, TILES, N], F32, name="out_sb")
-            for h in range(HALVES):
-                tiles = slice(h * HALF, (h + 1) * HALF)
-                for j in range(h * HALF, (h + 1) * HALF):
-                    nc.vector.tensor_tensor(out=out_sb[:, j, :], in0=accs[s][j][:], in1=bias[:], op=ALU.add)
-                nc.sync.dma_start(out=out_groups[s][:, tiles, :], in_=out_sb[:, tiles, :])
+        out_sbs = {}
+
+        def add_bias_and_store(s, h):
+            if h == 0:
+                out_sb = out_pool.tile([P, TILES, N], F32, name="out_sb")
+                out_sbs[s] = out_sb
+            tiles = slice(h * HALF, (h + 1) * HALF)
+            for j in range(h * HALF, (h + 1) * HALF):
+                nc.vector.tensor_tensor(out=out_sbs[s][:, j, :], in0=accs[s][j][:], in1=bias[:], op=ALU.add)
+            nc.sync.dma_start(out=out_groups[s][:, tiles, :], in_=out_sbs[s][:, tiles, :])
 
         gain = consts.tile([P, PLANES], F32)
         shift = consts.tile([P, PLANES], F32)
         bias = consts.tile([P, N], F32)
-        chunk_statistics(0)
+        ALL_CHUNKS = TILES * BN_CHUNKS
+        chunk_statistics(0, range(ALL_CHUNKS))
         nc.vector.tensor_copy(out=gain[:], in_=gain_bf[:].rearrange("p g t -> p (g t)"))
-        nc.vector.tensor_copy(out=shift[:], in_=shift_bf[:].rearrange("p g t -> p (g t)"))
         mean_and_variance(0)
         root(0)
-        nc.vector.tensor_copy(out=bias[:], in_=bias_bf[:])
+        nc.vector.tensor_copy(out=shift[:], in_=shift_bf[:].rearrange("p g t -> p (g t)"))
         invert_root(0)
+        nc.vector.tensor_copy(out=bias[:], in_=bias_bf[:])
+        offset(0)
         normalise(0)
-        chunk_statistics(1)
+        chunk_statistics(1, range(ALL_CHUNKS))
         mean_and_variance(1)
+        root(1)
 
         for s in range(GROUPS + LAG):
             if s >= LAG:
                 quantise(s - LAG)
-            if s < GROUPS:
-                planes = transpose_and_scale(s, 0)
-            if s + 1 < GROUPS:
-                root(s + 1)
-            if s >= LAG:
-                project(s - LAG)
-            if s < GROUPS:
-                regroup(s, 0, planes)
-                planes = transpose_and_scale(s, 1)
-                regroup(s, 1, planes)
-            if s + 2 < GROUPS:
-                chunk_statistics(s + 2)
             if s + 1 < GROUPS:
                 invert_root(s + 1)
             if s + 2 < GROUPS:
-                mean_and_variance(s + 2)
+                chunk_statistics(s + 2, range(0, 1))
+            if s + 1 < GROUPS:
+                offset(s + 1)
+            if s + 2 < GROUPS:
+                chunk_statistics(s + 2, range(1, ALL_CHUNKS))
+            if s < GROUPS:
+                planes = transpose_and_scale(s, 0)
+                regroup(s, 0, planes)
             if s + 1 < GROUPS:
                 normalise(s + 1)
             if s >= LAG:
-                add_bias_and_store(s - LAG)
+                project(s - LAG)
+            if s < GROUPS:
+                planes = transpose_and_scale(s, 1)
+                regroup(s, 1, planes)
+            if s >= LAG:
+                add_bias_and_store(s - LAG, 0)
+            if s + 2 < GROUPS:
+                mean_and_variance(s + 2)
+                root(s + 2)
+            if s >= LAG:
+                add_bias_and_store(s - LAG, 1)

@@ -20,9 +20,7 @@ D = 1024
 N = 512
 PASSES = D // K_PASS
 PLANES = PASSES * PACK
-TILES = 4
-GROUP_ROWS = TILES * P
-GROUPS = ROWS // GROUP_ROWS
+BANK = 512
 BN_CHUNK = 512
 BN_CHUNKS = D // BN_CHUNK
 BN_STATS_DIM = 6
@@ -31,46 +29,57 @@ EPS = 1e-5
 
 FLOPS = 2 * ROWS * D * N
 
-
+GROUP_TILES = (2, 2, 4, 4, 4, 4, 4, 4, 2, 2)
+GROUPS = len(GROUP_TILES)
+MAX_TILES = max(GROUP_TILES)
+assert sum(GROUP_TILES) * P == ROWS
+VECTOR_TILES = (2, 1, 1, 1, 1, 1, 1, 1, 0, 0)
+VECTOR_REGROUPS = ()
 LAG = 2
-HALVES = 2
-HALF = TILES // HALVES
-PIECES = 4
-PIECE_ROWS = GROUP_ROWS // PIECES
+DMA_TILES = 2
+PIECE_ROWS = 128
 
 
 def tile_stulayer_pa_t_kernel(tc, src, ln1_w, ln1_b, w_uvqk_words, w_uvqk_scales, b_uvqk, out):
     nc = tc.nc
-    src_groups = src.rearrange("t b d -> (t b) d").rearrange("(s p j) d -> s p j d", p=P, j=TILES)
-    out_groups = out.rearrange("t b n -> (t b) n").rearrange("(s p j) n -> s p j n", p=P, j=TILES)
+    src_rows = src.rearrange("t b d -> (t b) d")
+    out_rows = out.rearrange("t b n -> (t b) n")
+    src_groups = []
+    out_groups = []
+    first_row = 0
+    for n in GROUP_TILES:
+        rows = slice(first_row, first_row + n * P)
+        src_groups.append(src_rows[rows, :].rearrange("(p j) d -> p j d", j=n))
+        out_groups.append(out_rows[rows, :].rearrange("(p j) n -> p j n", j=n))
+        first_row += n * P
 
     with ExitStack() as ctx:
         consts = ctx.enter_context(tc.tile_pool(name="consts", bufs=1))
         x_pool = ctx.enter_context(tc.tile_pool(name="x", bufs=GROUPS))
-        small = ctx.enter_context(tc.tile_pool(name="small", bufs=5))
+        small = ctx.enter_context(tc.tile_pool(name="small", bufs=6))
         xhat_pool = ctx.enter_context(tc.tile_pool(name="xhat", bufs=3))
         plane_pool = ctx.enter_context(tc.tile_pool(name="planes", bufs=3))
         grouped_pool = ctx.enter_context(tc.tile_pool(name="grouped", bufs=PASSES * (LAG + 1)))
         mx_pool = ctx.enter_context(tc.tile_pool(name="mx", bufs=2))
         out_pool = ctx.enter_context(tc.tile_pool(name="outs", bufs=3))
         psum_t = ctx.enter_context(tc.psum_pool(name="psum_t", bufs=4))
-        psum_acc = ctx.enter_context(tc.psum_pool(name="psum_acc", bufs=TILES))
+        psum_acc = ctx.enter_context(tc.psum_pool(name="psum_acc", bufs=4))
         ctx.enter_context(tc.manual_schedule())
 
         w_scales = consts.tile([P, PASSES, N], U8, align_bytes=64)
         nc.vector.memset(w_scales[:].rearrange("p g n -> p (g n)").bitcast(I32), 0)
         x_tiles = []
-        for s in range(GROUPS):
-            x_sb = x_pool.tile([P, TILES, D], BF16, name="x_sb")
+        for u in range(GROUPS):
+            x_sb = x_pool.tile([P, GROUP_TILES[u], D], BF16, name="x_sb")
             x_tiles.append(x_sb)
 
-        def load(s):
-            for h in range(HALVES):
-                tiles = slice(h * HALF, (h + 1) * HALF)
-                nc.sync.dma_start(out=x_tiles[s][:, tiles, :], in_=src_groups[s][:, tiles, :])
+        def load(u, step):
+            for j in range(0, GROUP_TILES[u], step):
+                nc.sync.dma_start(out=x_tiles[u][:, j : j + step, :], in_=src_groups[u][:, j : j + step, :])
 
-        load(0)
-        load(1)
+        load(0, 1)
+        load(1, DMA_TILES)
+        load(2, DMA_TILES)
         for g in range(PASSES):
             for quadrant in range(4):
                 nc.sync.dma_start(
@@ -83,8 +92,8 @@ def tile_stulayer_pa_t_kernel(tc, src, ln1_w, ln1_b, w_uvqk_words, w_uvqk_scales
                 out=w_words[:, g, :].bitcast(I32),
                 in_=w_uvqk_words[g].rearrange("p n t -> p (n t)").bitcast(I32),
             )
-        for s in range(2, GROUPS):
-            load(s)
+        for u in range(3, GROUPS):
+            load(u, DMA_TILES)
 
         gain_bf = consts.tile([P, PASSES, PACK], BF16)
         shift_bf = consts.tile([P, PASSES, PACK], BF16)
@@ -100,6 +109,9 @@ def tile_stulayer_pa_t_kernel(tc, src, ln1_w, ln1_b, w_uvqk_words, w_uvqk_scales
         nc.vector.memset(eps[:], EPS)
         warm = consts.tile([P, 1], F32)
         nc.scalar.activation(out=warm[:], in_=eps[:], func=ACT.Sqrt)
+        gain = consts.tile([P, PLANES], F32)
+        shift = consts.tile([P, PLANES], F32)
+        bias = consts.tile([P, N], F32)
 
         chunk_stats = {}
         mean_vars = {}
@@ -110,72 +122,107 @@ def tile_stulayer_pa_t_kernel(tc, src, ln1_w, ln1_b, w_uvqk_words, w_uvqk_scales
         groupeds = {}
         operands = {}
         accs = {}
+        out_sbs = {}
 
-        def chunk_statistics(s, chunks):
-            if s not in chunk_stats:
-                stats = small.tile([P, TILES, BN_CHUNKS, BN_STATS_DIM], F32, name="stats")
-                chunk_stats[s] = stats
+        def chunk_statistics(u, chunks):
+            if u not in chunk_stats:
+                stats = small.tile([P, MAX_TILES, BN_CHUNKS, BN_STATS_DIM], F32, name="stats")
+                chunk_stats[u] = stats
             for i in chunks:
                 j, c = divmod(i, BN_CHUNKS)
                 nc.vector.bn_stats(
-                    out=chunk_stats[s][:, j, c, :], in_=x_tiles[s][:, j, c * BN_CHUNK : (c + 1) * BN_CHUNK]
+                    out=chunk_stats[u][:, j, c, :], in_=x_tiles[u][:, j, c * BN_CHUNK : (c + 1) * BN_CHUNK]
                 )
 
-        def mean_and_variance(s):
-            mean_var = small.tile([P, TILES, BN_AGGR_DIM], F32, name="mean_var")
-            for j in range(TILES):
-                nc.vector.bn_aggr(out=mean_var[:, j, :], in_=chunk_stats[s][:, j].rearrange("p c v -> p (c v)"))
-            mean_vars[s] = mean_var
+        def mean_and_variance(u):
+            mean_var = small.tile([P, MAX_TILES, BN_AGGR_DIM], F32, name="mean_var")
+            for j in range(GROUP_TILES[u]):
+                nc.vector.bn_aggr(out=mean_var[:, j, :], in_=chunk_stats[u][:, j].rearrange("p c v -> p (c v)"))
+            mean_vars[u] = mean_var
 
-        def root(s):
-            std = small.tile([P, TILES], F32, name="std")
-            nc.scalar.activation(out=std[:], in_=mean_vars[s][:, :, 1], func=ACT.Sqrt, bias=eps[:], scale=1.0)
-            stds[s] = std
+        def root(u):
+            n = GROUP_TILES[u]
+            std = small.tile([P, MAX_TILES], F32, name="std")
+            nc.scalar.activation(out=std[:, :n], in_=mean_vars[u][:, :n, 1], func=ACT.Sqrt, bias=eps[:], scale=1.0)
+            stds[u] = std
 
-        def invert_root(s):
-            rstd = small.tile([P, TILES], F32, name="rstd")
-            nc.vector.reciprocal(out=rstd[:], in_=stds[s][:])
-            rstds[s] = rstd
+        def invert_root(u):
+            n = GROUP_TILES[u]
+            rstd = small.tile([P, MAX_TILES], F32, name="rstd")
+            nc.vector.reciprocal(out=rstd[:, :n], in_=stds[u][:, :n])
+            rstds[u] = rstd
 
-        def offset(s):
-            off = small.tile([P, TILES], F32, name="off")
+        def offset(u):
+            n = GROUP_TILES[u]
+            off = small.tile([P, MAX_TILES], F32, name="off")
             nc.vector.scalar_tensor_tensor(
-                out=off[:], in0=mean_vars[s][:, :, 0], scalar=-1.0, in1=rstds[s][:], op0=ALU.mult, op1=ALU.mult
+                out=off[:, :n], in0=mean_vars[u][:, :n, 0], scalar=-1.0, in1=rstds[u][:, :n], op0=ALU.mult, op1=ALU.mult
             )
-            offsets[s] = off
+            offsets[u] = off
 
-        def normalise(s):
-            xhat = xhat_pool.tile([P, TILES, PLANES, P], F32, name="xhat")
-            for j in range(TILES):
-                nc.scalar.activation(
-                    out=xhat[:, j].rearrange("p (g t) q -> p g t q", t=PACK),
-                    in_=x_tiles[s][:, j, :].rearrange("p (g q t) -> p g t q", q=P, t=PACK),
-                    func=ACT.Identity,
-                    scale=rstds[s][:, j : j + 1],
-                    bias=offsets[s][:, j : j + 1],
-                )
-            xhats[s] = xhat
+        def normalise(u, on_vector):
+            if u not in xhats:
+                xhat = xhat_pool.tile([P, MAX_TILES, PLANES, P], F32, name="xhat")
+                xhats[u] = xhat
+            xhat = xhats[u]
+            split = GROUP_TILES[u] - VECTOR_TILES[u]
+            for j in range(split, GROUP_TILES[u]) if on_vector else range(split):
+                sorted_out = xhat[:, j].rearrange("p (g t) q -> p g t q", t=PACK)
+                sorted_in = x_tiles[u][:, j, :].rearrange("p (g q t) -> p g t q", q=P, t=PACK)
+                if on_vector:
+                    nc.vector.tensor_scalar(
+                        out=sorted_out,
+                        in0=sorted_in,
+                        scalar1=mean_vars[u][:, j, 0:1],
+                        scalar2=rstds[u][:, j : j + 1],
+                        op0=ALU.subtract,
+                        op1=ALU.mult,
+                    )
+                else:
+                    nc.scalar.activation(
+                        out=sorted_out,
+                        in_=sorted_in,
+                        func=ACT.Identity,
+                        scale=rstds[u][:, j : j + 1],
+                        bias=offsets[u][:, j : j + 1],
+                    )
 
-        def transpose_and_scale(s, g):
-            planes = plane_pool.tile([P, PACK, GROUP_ROWS], BF16, name="planes")
-            for t in range(PACK):
-                plane = g * PACK + t
-                xt = psum_t.tile([P, GROUP_ROWS], F32, name="xt")
-                for j in range(TILES):
-                    nc.tensor.transpose(xt[:, j * P : (j + 1) * P], xhats[s][:, j, plane, :], identity[:])
-                nc.scalar.activation(
-                    out=planes[:, t, :],
-                    in_=xt[:],
-                    func=ACT.Identity,
-                    scale=gain[:, plane : plane + 1],
-                    bias=shift[:, plane : plane + 1],
-                )
+        def transpose_and_scale(u, g):
+            n = GROUP_TILES[u]
+            width = n * P
+            planes = plane_pool.tile([P, PACK, MAX_TILES * P], BF16, name="planes")
+            in_bank = BANK // width
+            for t0 in range(0, PACK, in_bank):
+                xt = psum_t.tile([P, BANK], F32, name="xt")
+                for i in range(in_bank):
+                    for j in range(n):
+                        nc.tensor.transpose(
+                            xt[:, i * width + j * P : i * width + (j + 1) * P],
+                            xhats[u][:, j, g * PACK + t0 + i, :],
+                            identity[:],
+                        )
+                for i in range(in_bank):
+                    plane = g * PACK + t0 + i
+                    nc.scalar.activation(
+                        out=planes[:, t0 + i, :width],
+                        in_=xt[:, i * width : (i + 1) * width],
+                        func=ACT.Identity,
+                        scale=gain[:, plane : plane + 1],
+                        bias=shift[:, plane : plane + 1],
+                    )
             return planes
 
-        def regroup(s, g, planes):
-            grouped = grouped_pool.tile([P, GROUP_ROWS, PACK], BF16, align_bytes=64, name="grouped")
-            for i in range(PIECES):
-                rows = slice(i * PIECE_ROWS, (i + 1) * PIECE_ROWS)
+        def regroup(u, g, planes):
+            grouped = grouped_pool.tile([P, MAX_TILES * P, PACK], BF16, align_bytes=64, name="grouped")
+            groupeds[u, g] = grouped
+            if (u, g) in VECTOR_REGROUPS:
+                width = GROUP_TILES[u] * P
+                nc.vector.tensor_copy(
+                    out=grouped[:, :width, :], in_=planes[:, :, :width].rearrange("p t r -> p r t")
+                )
+                return
+            for r0 in range(0, GROUP_TILES[u] * P, PIECE_ROWS):
+                rows = slice(r0, r0 + PIECE_ROWS)
                 nc.gpsimd.tensor_scalar(
                     out=grouped[:, rows, :],
                     in0=planes[:, :, rows].rearrange("p t r -> p r t"),
@@ -184,30 +231,33 @@ def tile_stulayer_pa_t_kernel(tc, src, ln1_w, ln1_b, w_uvqk_words, w_uvqk_scales
                     op0=ALU.mult,
                     op1=ALU.add,
                 )
-            groupeds[s, g] = grouped
+            groupeds[u, g] = grouped
 
-        def quantise(s):
-            codes = mx_pool.tile([P, PASSES, GROUP_ROWS], U32, align_bytes=64, name="codes")
-            scales = mx_pool.tile([P, PASSES, GROUP_ROWS], U8, align_bytes=64, name="scales")
-            for g in range(PASSES):
-                nc.vector.quantize_mx(
-                    out=codes[:, g, :].bitcast(FP8X4),
-                    scales=scales[:, g, :],
-                    in_=groupeds[s, g][:].rearrange("p r t -> p (r t)"),
-                )
-            operands[s] = (codes, scales)
+        def quantise(u, g):
+            width = GROUP_TILES[u] * P
+            if u not in operands:
+                codes = mx_pool.tile([P, PASSES, MAX_TILES * P], U32, align_bytes=64, name="codes")
+                scales = mx_pool.tile([P, PASSES, MAX_TILES * P], U8, align_bytes=64, name="scales")
+                operands[u] = (codes, scales)
+            codes, scales = operands[u]
+            nc.vector.quantize_mx(
+                out=codes[:, g, :width].bitcast(FP8X4),
+                scales=scales[:, g, :width],
+                in_=groupeds[u, g][:, :width, :].rearrange("p r t -> p (r t)"),
+            )
 
-        def project(s):
-            codes, scales = operands[s]
-            accs[s] = []
-            for j in range(TILES):
-                acc = psum_acc.tile([P, N], F32, name="acc")
-                accs[s].append(acc)
-            for g in range(PASSES):
-                for j in range(TILES):
+        def project(u, passes):
+            codes, scales = operands[u]
+            if u not in accs:
+                accs[u] = []
+                for j in range(GROUP_TILES[u]):
+                    acc = psum_acc.tile([P, N], F32, name="acc")
+                    accs[u].append(acc)
+            for g in passes:
+                for j in range(GROUP_TILES[u]):
                     rows = slice(j * P, (j + 1) * P)
                     nc.tensor.matmul_mx(
-                        out=accs[s][j][:],
+                        out=accs[u][j][:],
                         lhsT=codes[:, g, rows].bitcast(FP8X4),
                         lhsT_scale=scales[:, g, rows],
                         rhs=w_words[:, g, :].bitcast(FP8X4),
@@ -216,59 +266,81 @@ def tile_stulayer_pa_t_kernel(tc, src, ln1_w, ln1_b, w_uvqk_words, w_uvqk_scales
                         stop=(g == PASSES - 1),
                     )
 
-        out_sbs = {}
+        def add_bias_and_store(u, j0):
+            if j0 == 0:
+                out_sb = out_pool.tile([P, MAX_TILES, N], F32, name="out_sb")
+                out_sbs[u] = out_sb
+            tiles = slice(j0, j0 + DMA_TILES)
+            for j in range(j0, j0 + DMA_TILES):
+                nc.vector.tensor_tensor(out=out_sbs[u][:, j, :], in0=accs[u][j][:], in1=bias[:], op=ALU.add)
+            nc.sync.dma_start(out=out_groups[u][:, tiles, :], in_=out_sbs[u][:, tiles, :])
 
-        def add_bias_and_store(s, h):
-            if h == 0:
-                out_sb = out_pool.tile([P, TILES, N], F32, name="out_sb")
-                out_sbs[s] = out_sb
-            tiles = slice(h * HALF, (h + 1) * HALF)
-            for j in range(h * HALF, (h + 1) * HALF):
-                nc.vector.tensor_tensor(out=out_sbs[s][:, j, :], in0=accs[s][j][:], in1=bias[:], op=ALU.add)
-            nc.sync.dma_start(out=out_groups[s][:, tiles, :], in_=out_sbs[s][:, tiles, :])
+        def chunks(u):
+            return GROUP_TILES[u] * BN_CHUNKS
 
-        gain = consts.tile([P, PLANES], F32)
-        shift = consts.tile([P, PLANES], F32)
-        bias = consts.tile([P, N], F32)
-        ALL_CHUNKS = TILES * BN_CHUNKS
-        chunk_statistics(0, range(ALL_CHUNKS))
+        chunk_statistics(0, range(chunks(0)))
         nc.vector.tensor_copy(out=gain[:], in_=gain_bf[:].rearrange("p g t -> p (g t)"))
         mean_and_variance(0)
         root(0)
-        nc.vector.tensor_copy(out=shift[:], in_=shift_bf[:].rearrange("p g t -> p (g t)"))
+        chunk_statistics(1, range(0, 1))
         invert_root(0)
+        nc.vector.tensor_copy(out=shift[:], in_=shift_bf[:].rearrange("p g t -> p (g t)"))
+        normalise(0, True)
+        chunk_statistics(1, range(1, chunks(1)))
         nc.vector.tensor_copy(out=bias[:], in_=bias_bf[:])
-        offset(0)
-        normalise(0)
-        chunk_statistics(1, range(ALL_CHUNKS))
         mean_and_variance(1)
-        root(1)
 
-        for s in range(GROUPS + LAG):
+        for s in range(GROUPS):
             if s >= LAG:
-                quantise(s - LAG)
+                quantise(s - LAG, 0)
+                quantise(s - LAG, 1)
+            if s == 0:
+                planes = transpose_and_scale(0, 0)
+                regroup(0, 0, planes)
+                root(1)
+                chunk_statistics(2, range(0, 2))
+                invert_root(1)
+                chunk_statistics(2, range(2, 3))
+                offset(1)
+                normalise(1, True)
+                chunk_statistics(2, range(3, chunks(2)))
+                planes = transpose_and_scale(0, 1)
+                regroup(0, 1, planes)
+                normalise(1, False)
+                mean_and_variance(2)
+                root(2)
+                continue
             if s + 1 < GROUPS:
                 invert_root(s + 1)
             if s + 2 < GROUPS:
                 chunk_statistics(s + 2, range(0, 1))
             if s + 1 < GROUPS:
                 offset(s + 1)
+                normalise(s + 1, True)
             if s + 2 < GROUPS:
-                chunk_statistics(s + 2, range(1, ALL_CHUNKS))
-            if s < GROUPS:
-                planes = transpose_and_scale(s, 0)
-                regroup(s, 0, planes)
+                chunk_statistics(s + 2, range(1, chunks(s + 2)))
+            planes = transpose_and_scale(s, 0)
+            regroup(s, 0, planes)
             if s + 1 < GROUPS:
-                normalise(s + 1)
+                normalise(s + 1, False)
             if s >= LAG:
-                project(s - LAG)
-            if s < GROUPS:
-                planes = transpose_and_scale(s, 1)
-                regroup(s, 1, planes)
+                project(s - LAG, range(PASSES))
+            planes = transpose_and_scale(s, 1)
+            regroup(s, 1, planes)
             if s >= LAG:
                 add_bias_and_store(s - LAG, 0)
             if s + 2 < GROUPS:
                 mean_and_variance(s + 2)
                 root(s + 2)
-            if s >= LAG:
-                add_bias_and_store(s - LAG, 1)
+            if s >= LAG and GROUP_TILES[s - LAG] > DMA_TILES:
+                add_bias_and_store(s - LAG, DMA_TILES)
+        before_last, last = GROUPS - 2, GROUPS - 1
+        quantise(before_last, 0)
+        quantise(before_last, 1)
+        project(before_last, range(PASSES))
+        quantise(last, 0)
+        project(last, range(0, 1))
+        add_bias_and_store(before_last, 0)
+        quantise(last, 1)
+        project(last, range(1, PASSES))
+        add_bias_and_store(last, 0)

@@ -34,7 +34,6 @@ GROUPS = len(GROUP_TILES)
 MAX_TILES = max(GROUP_TILES)
 assert sum(GROUP_TILES) * P == ROWS
 VECTOR_TILES = (2, 1, 1, 1, 1, 1, 1, 1, 0, 0)
-VECTOR_REGROUPS = ()
 LAG = 2
 DMA_TILES = 2
 PIECE_ROWS = 128
@@ -73,9 +72,9 @@ def tile_stulayer_pa_t_kernel(tc, src, ln1_w, ln1_b, w_uvqk_words, w_uvqk_scales
             x_sb = x_pool.tile([P, GROUP_TILES[u], D], BF16, name="x_sb")
             x_tiles.append(x_sb)
 
-        def load(u, step):
-            for j in range(0, GROUP_TILES[u], step):
-                nc.sync.dma_start(out=x_tiles[u][:, j : j + step, :], in_=src_groups[u][:, j : j + step, :])
+        def load(u, tiles):
+            for j in range(0, GROUP_TILES[u], tiles):
+                nc.sync.dma_start(out=x_tiles[u][:, j : j + tiles, :], in_=src_groups[u][:, j : j + tiles, :])
 
         load(0, 1)
         load(1, DMA_TILES)
@@ -124,11 +123,14 @@ def tile_stulayer_pa_t_kernel(tc, src, ln1_w, ln1_b, w_uvqk_words, w_uvqk_scales
         accs = {}
         out_sbs = {}
 
-        def chunk_statistics(u, chunks):
+        def half_rows(u):
+            return GROUP_TILES[u] * BN_CHUNKS
+
+        def chunk_statistics(u, halves):
             if u not in chunk_stats:
                 stats = small.tile([P, MAX_TILES, BN_CHUNKS, BN_STATS_DIM], F32, name="stats")
                 chunk_stats[u] = stats
-            for i in chunks:
+            for i in halves:
                 j, c = divmod(i, BN_CHUNKS)
                 nc.vector.bn_stats(
                     out=chunk_stats[u][:, j, c, :], in_=x_tiles[u][:, j, c * BN_CHUNK : (c + 1) * BN_CHUNK]
@@ -214,18 +216,11 @@ def tile_stulayer_pa_t_kernel(tc, src, ln1_w, ln1_b, w_uvqk_words, w_uvqk_scales
 
         def regroup(u, g, planes):
             grouped = grouped_pool.tile([P, MAX_TILES * P, PACK], BF16, align_bytes=64, name="grouped")
-            groupeds[u, g] = grouped
-            if (u, g) in VECTOR_REGROUPS:
-                width = GROUP_TILES[u] * P
-                nc.vector.tensor_copy(
-                    out=grouped[:, :width, :], in_=planes[:, :, :width].rearrange("p t r -> p r t")
-                )
-                return
             for r0 in range(0, GROUP_TILES[u] * P, PIECE_ROWS):
-                rows = slice(r0, r0 + PIECE_ROWS)
+                piece = slice(r0, r0 + PIECE_ROWS)
                 nc.gpsimd.tensor_scalar(
-                    out=grouped[:, rows, :],
-                    in0=planes[:, :, rows].rearrange("p t r -> p r t"),
+                    out=grouped[:, piece, :].rearrange("p (c i) t -> p c t i", i=4),
+                    in0=planes[:, :, piece].rearrange("p t (c i) -> p c t i", i=4),
                     scalar1=1.0,
                     scalar2=0.0,
                     op0=ALU.mult,
@@ -255,11 +250,11 @@ def tile_stulayer_pa_t_kernel(tc, src, ln1_w, ln1_b, w_uvqk_words, w_uvqk_scales
                     accs[u].append(acc)
             for g in passes:
                 for j in range(GROUP_TILES[u]):
-                    rows = slice(j * P, (j + 1) * P)
+                    columns = slice(j * P, (j + 1) * P)
                     nc.tensor.matmul_mx(
                         out=accs[u][j][:],
-                        lhsT=codes[:, g, rows].bitcast(FP8X4),
-                        lhsT_scale=scales[:, g, rows],
+                        lhsT=codes[:, g, columns].bitcast(FP8X4),
+                        lhsT_scale=scales[:, g, columns],
                         rhs=w_words[:, g, :].bitcast(FP8X4),
                         rhs_scale=w_scales[:, g, :],
                         start=(g == 0),
@@ -275,10 +270,7 @@ def tile_stulayer_pa_t_kernel(tc, src, ln1_w, ln1_b, w_uvqk_words, w_uvqk_scales
                 nc.vector.tensor_tensor(out=out_sbs[u][:, j, :], in0=accs[u][j][:], in1=bias[:], op=ALU.add)
             nc.sync.dma_start(out=out_groups[u][:, tiles, :], in_=out_sbs[u][:, tiles, :])
 
-        def chunks(u):
-            return GROUP_TILES[u] * BN_CHUNKS
-
-        chunk_statistics(0, range(chunks(0)))
+        chunk_statistics(0, range(half_rows(0)))
         nc.vector.tensor_copy(out=gain[:], in_=gain_bf[:].rearrange("p g t -> p (g t)"))
         mean_and_variance(0)
         root(0)
@@ -286,30 +278,29 @@ def tile_stulayer_pa_t_kernel(tc, src, ln1_w, ln1_b, w_uvqk_words, w_uvqk_scales
         invert_root(0)
         nc.vector.tensor_copy(out=shift[:], in_=shift_bf[:].rearrange("p g t -> p (g t)"))
         normalise(0, True)
-        chunk_statistics(1, range(1, chunks(1)))
+        chunk_statistics(1, range(1, half_rows(1)))
         nc.vector.tensor_copy(out=bias[:], in_=bias_bf[:])
         mean_and_variance(1)
+        planes = transpose_and_scale(0, 0)
+        regroup(0, 0, planes)
+        root(1)
+        chunk_statistics(2, range(0, 2))
+        invert_root(1)
+        chunk_statistics(2, range(2, 3))
+        offset(1)
+        normalise(1, True)
+        chunk_statistics(2, range(3, half_rows(2)))
+        planes = transpose_and_scale(0, 1)
+        regroup(0, 1, planes)
+        normalise(1, False)
+        mean_and_variance(2)
+        root(2)
 
-        for s in range(GROUPS):
-            if s >= LAG:
-                quantise(s - LAG, 0)
-                quantise(s - LAG, 1)
-            if s == 0:
-                planes = transpose_and_scale(0, 0)
-                regroup(0, 0, planes)
-                root(1)
-                chunk_statistics(2, range(0, 2))
-                invert_root(1)
-                chunk_statistics(2, range(2, 3))
-                offset(1)
-                normalise(1, True)
-                chunk_statistics(2, range(3, chunks(2)))
-                planes = transpose_and_scale(0, 1)
-                regroup(0, 1, planes)
-                normalise(1, False)
-                mean_and_variance(2)
-                root(2)
-                continue
+        for s in range(1, GROUPS):
+            done = s - LAG
+            if done >= 0:
+                quantise(done, 0)
+                quantise(done, 1)
             if s + 1 < GROUPS:
                 invert_root(s + 1)
             if s + 2 < GROUPS:
@@ -318,22 +309,23 @@ def tile_stulayer_pa_t_kernel(tc, src, ln1_w, ln1_b, w_uvqk_words, w_uvqk_scales
                 offset(s + 1)
                 normalise(s + 1, True)
             if s + 2 < GROUPS:
-                chunk_statistics(s + 2, range(1, chunks(s + 2)))
+                chunk_statistics(s + 2, range(1, half_rows(s + 2)))
             planes = transpose_and_scale(s, 0)
             regroup(s, 0, planes)
             if s + 1 < GROUPS:
                 normalise(s + 1, False)
-            if s >= LAG:
-                project(s - LAG, range(PASSES))
+            if done >= 0:
+                project(done, range(PASSES))
             planes = transpose_and_scale(s, 1)
             regroup(s, 1, planes)
-            if s >= LAG:
-                add_bias_and_store(s - LAG, 0)
+            if done >= 0:
+                add_bias_and_store(done, 0)
             if s + 2 < GROUPS:
                 mean_and_variance(s + 2)
                 root(s + 2)
-            if s >= LAG and GROUP_TILES[s - LAG] > DMA_TILES:
-                add_bias_and_store(s - LAG, DMA_TILES)
+            if done >= 0 and GROUP_TILES[done] > DMA_TILES:
+                add_bias_and_store(done, DMA_TILES)
+
         before_last, last = GROUPS - 2, GROUPS - 1
         quantise(before_last, 0)
         quantise(before_last, 1)

@@ -181,13 +181,16 @@ def tile_stulayer_pa_t_kernel(tc, src, ln1_w, ln1_b, w_uvqk_words, w_uvqk_scales
                         op1=ALU.mult,
                     )
                 else:
-                    nc.scalar.activation(
-                        out=sorted_out,
-                        in_=sorted_in,
-                        func=ACT.Identity,
-                        scale=rstds[u][:, j : j + 1],
-                        bias=offsets[u][:, j : j + 1],
-                    )
+                    for g in range(PASSES):
+                        nc.scalar.activation(
+                            out=xhat[:, j, g * PACK : (g + 1) * PACK, :].rearrange("p t (c i) -> p c t i", i=4),
+                            in_=x_tiles[u][:, j, g * K_PASS : (g + 1) * K_PASS].rearrange(
+                                "p (c i t) -> p c t i", i=4, t=PACK
+                            ),
+                            func=ACT.Identity,
+                            scale=rstds[u][:, j : j + 1],
+                            bias=offsets[u][:, j : j + 1],
+                        )
 
         def transpose_and_scale(u, g):
             n = GROUP_TILES[u]

@@ -67,6 +67,10 @@ def tile_stulayer_pa_t_kernel(tc, src, ln1_w, ln1_b, w_uvqk_words, w_uvqk_scales
 
         w_scales = consts.tile([P, PASSES, N], U8, align_bytes=64)
         nc.vector.memset(w_scales[:].rearrange("p g n -> p (g n)").bitcast(I32), 0)
+        bias_row = consts.tile([P, N], BF16)
+        nc.vector.memset(bias_row[:], 0.0)
+        ones = consts.tile([P, P], BF16)
+        nc.vector.memset(ones[:], 1.0)
         x_tiles = []
         for u in range(GROUPS):
             x_sb = x_pool.tile([P, GROUP_TILES[u], D], BF16, name="x_sb")
@@ -99,8 +103,7 @@ def tile_stulayer_pa_t_kernel(tc, src, ln1_w, ln1_b, w_uvqk_words, w_uvqk_scales
         with nc.allow_non_contiguous_dma(reason="2 KiB vectors in runs of four features"):
             nc.scalar.dma_start(out=gain_bf[:], in_=ln1_w.rearrange("(g p t) -> p g t", p=P, t=PACK))
             nc.scalar.dma_start(out=shift_bf[:], in_=ln1_b.rearrange("(g p t) -> p g t", p=P, t=PACK))
-        bias_bf = consts.tile([P, N], BF16)
-        nc.scalar.dma_start(out=bias_bf[:], in_=b_uvqk.partition_broadcast(P))
+        nc.scalar.dma_start(out=bias_row[0:1, :], in_=b_uvqk.rearrange("(o n) -> o n", o=1))
 
         identity = consts.tile([P, P], F32)
         make_identity(nc, identity[:])
@@ -282,7 +285,6 @@ def tile_stulayer_pa_t_kernel(tc, src, ln1_w, ln1_b, w_uvqk_words, w_uvqk_scales
         nc.vector.tensor_copy(out=shift[:], in_=shift_bf[:].rearrange("p g t -> p (g t)"))
         normalise(0, True)
         chunk_statistics(1, range(1, half_rows(1)))
-        nc.vector.tensor_copy(out=bias[:], in_=bias_bf[:])
         mean_and_variance(1)
         planes = transpose_and_scale(0, 0)
         regroup(0, 0, planes)
@@ -298,6 +300,9 @@ def tile_stulayer_pa_t_kernel(tc, src, ln1_w, ln1_b, w_uvqk_words, w_uvqk_scales
         normalise(1, False)
         mean_and_variance(2)
         root(2)
+        bias_sum = psum_acc.tile([P, N], F32, name="acc")
+        nc.tensor.matmul(out=bias_sum[:], lhsT=ones[:], rhs=bias_row[:], start=True, stop=True)
+        nc.scalar.copy(out=bias[:], in_=bias_sum[:])
 
         for s in range(1, GROUPS):
             done = s - LAG

@@ -82,7 +82,13 @@ def tile_stulayer_pa_t_kernel(tc, src, ln1_w, ln1_b, w_uvqk_words, w_uvqk_scales
 
         load(0, 1)
         load(1, DMA_TILES)
+        gain_bf = consts.tile([P, PASSES, PACK], BF16)
+        shift_bf = consts.tile([P, PASSES, PACK], BF16)
+        with nc.allow_non_contiguous_dma(reason="2 KiB vectors in runs of four features"):
+            nc.sync.dma_start(out=gain_bf[:], in_=ln1_w.rearrange("(g p t) -> p g t", p=P, t=PACK))
+            nc.sync.dma_start(out=shift_bf[:], in_=ln1_b.rearrange("(g p t) -> p g t", p=P, t=PACK))
         load(2, DMA_TILES)
+        load(3, DMA_TILES)
         for g in range(PASSES):
             for quadrant in range(4):
                 nc.sync.dma_start(
@@ -95,14 +101,9 @@ def tile_stulayer_pa_t_kernel(tc, src, ln1_w, ln1_b, w_uvqk_words, w_uvqk_scales
                 out=w_words[:, g, :].bitcast(I32),
                 in_=w_uvqk_words[g].rearrange("p n t -> p (n t)").bitcast(I32),
             )
-        for u in range(3, GROUPS):
+        for u in range(4, GROUPS):
             load(u, DMA_TILES)
 
-        gain_bf = consts.tile([P, PASSES, PACK], BF16)
-        shift_bf = consts.tile([P, PASSES, PACK], BF16)
-        with nc.allow_non_contiguous_dma(reason="2 KiB vectors in runs of four features"):
-            nc.scalar.dma_start(out=gain_bf[:], in_=ln1_w.rearrange("(g p t) -> p g t", p=P, t=PACK))
-            nc.scalar.dma_start(out=shift_bf[:], in_=ln1_b.rearrange("(g p t) -> p g t", p=P, t=PACK))
         nc.scalar.dma_start(out=bias_row[0:1, :], in_=b_uvqk.rearrange("(o n) -> o n", o=1))
 
         identity = consts.tile([P, P], F32)
@@ -267,24 +268,25 @@ def tile_stulayer_pa_t_kernel(tc, src, ln1_w, ln1_b, w_uvqk_words, w_uvqk_scales
                         stop=(g == PASSES - 1),
                     )
 
-        def add_bias_and_store(u, j0):
+        def add_bias_and_store(u, j0, count):
             if j0 == 0:
                 out_sb = out_pool.tile([P, MAX_TILES, N], F32, name="out_sb")
                 out_sbs[u] = out_sb
-            tiles = slice(j0, j0 + DMA_TILES)
-            for j in range(j0, j0 + DMA_TILES):
+            tiles = slice(j0, j0 + count)
+            for j in range(j0, j0 + count):
                 nc.vector.tensor_tensor(out=out_sbs[u][:, j, :], in0=accs[u][j][:], in1=bias[:], op=ALU.add)
             nc.sync.dma_start(out=out_groups[u][:, tiles, :], in_=out_sbs[u][:, tiles, :])
 
         chunk_statistics(0, range(half_rows(0)))
-        nc.vector.tensor_copy(out=gain[:], in_=gain_bf[:].rearrange("p g t -> p (g t)"))
         mean_and_variance(0)
         root(0)
+        nc.scalar.copy(out=gain[:], in_=gain_bf[:].rearrange("p g t -> p (g t)"))
+        nc.scalar.copy(out=shift[:], in_=shift_bf[:].rearrange("p g t -> p (g t)"))
         chunk_statistics(1, range(0, 1))
         invert_root(0)
-        nc.vector.tensor_copy(out=shift[:], in_=shift_bf[:].rearrange("p g t -> p (g t)"))
+        chunk_statistics(1, range(1, 2))
         normalise(0, True)
-        chunk_statistics(1, range(1, half_rows(1)))
+        chunk_statistics(1, range(2, half_rows(1)))
         mean_and_variance(1)
         planes = transpose_and_scale(0, 0)
         regroup(0, 0, planes)
@@ -327,12 +329,12 @@ def tile_stulayer_pa_t_kernel(tc, src, ln1_w, ln1_b, w_uvqk_words, w_uvqk_scales
             planes = transpose_and_scale(s, 1)
             regroup(s, 1, planes)
             if done >= 0:
-                add_bias_and_store(done, 0)
+                add_bias_and_store(done, 0, DMA_TILES)
             if s + 2 < GROUPS:
                 mean_and_variance(s + 2)
                 root(s + 2)
             if done >= 0 and GROUP_TILES[done] > DMA_TILES:
-                add_bias_and_store(done, DMA_TILES)
+                add_bias_and_store(done, DMA_TILES, DMA_TILES)
 
         before_last, last = GROUPS - 2, GROUPS - 1
         quantise(before_last, 0)
@@ -340,7 +342,8 @@ def tile_stulayer_pa_t_kernel(tc, src, ln1_w, ln1_b, w_uvqk_words, w_uvqk_scales
         project(before_last, range(PASSES))
         quantise(last, 0)
         project(last, range(0, 1))
-        add_bias_and_store(before_last, 0)
+        add_bias_and_store(before_last, 0, DMA_TILES)
         quantise(last, 1)
         project(last, range(1, PASSES))
-        add_bias_and_store(last, 0)
+        for j in range(GROUP_TILES[last]):
+            add_bias_and_store(last, j, 1)

@@ -36,7 +36,7 @@ assert sum(GROUP_TILES) * P == ROWS
 VECTOR_TILES = (2, 1, 1, 1, 1, 1, 1, 1, 0, 0)
 LAG = 2
 DMA_TILES = 2
-PIECE_ROWS = 128
+PIECE_ROWS = 256
 
 
 def tile_stulayer_pa_t_kernel(tc, src, ln1_w, ln1_b, w_uvqk_words, w_uvqk_scales, b_uvqk, out):
@@ -306,41 +306,40 @@ def tile_stulayer_pa_t_kernel(tc, src, ln1_w, ln1_b, w_uvqk_words, w_uvqk_scales
         nc.tensor.matmul(out=bias_sum[:], lhsT=ones[:], rhs=bias_row[:], start=True, stop=True)
         nc.scalar.copy(out=bias[:], in_=bias_sum[:])
 
+        chunk_statistics(3, range(0, 2))
+        invert_root(2)
+        quantise(0, 0)
+        offset(2)
+        normalise(2, True)
+
         for s in range(1, GROUPS):
             done = s - LAG
-            if done >= 0:
-                quantise(done, 0)
-                quantise(done, 1)
-            if s + 1 < GROUPS:
-                invert_root(s + 1)
             if s + 2 < GROUPS:
-                chunk_statistics(s + 2, range(0, 1))
-            if s + 1 < GROUPS:
-                offset(s + 1)
-                normalise(s + 1, True)
-            if s + 2 < GROUPS:
-                chunk_statistics(s + 2, range(1, half_rows(s + 2)))
+                chunk_statistics(s + 2, range(2 if s == 1 else 0, half_rows(s + 2)))
+                mean_and_variance(s + 2)
             planes = transpose_and_scale(s, 0)
             regroup(s, 0, planes)
             if s + 1 < GROUPS:
                 normalise(s + 1, False)
+            if s + 2 < GROUPS:
+                root(s + 2)
             if done >= 0:
                 project(done, range(PASSES))
+                add_bias_and_store(done, 0, DMA_TILES)
+                if GROUP_TILES[done] > DMA_TILES:
+                    add_bias_and_store(done, DMA_TILES, DMA_TILES)
+            quantise(s - 1, 1)
+            if s + 2 < GROUPS:
+                invert_root(s + 2)
+            quantise(s, 0)
+            if s + 2 < GROUPS:
+                offset(s + 2)
+                normalise(s + 2, True)
             planes = transpose_and_scale(s, 1)
             regroup(s, 1, planes)
-            if done >= 0:
-                add_bias_and_store(done, 0, DMA_TILES)
-            if s + 2 < GROUPS:
-                mean_and_variance(s + 2)
-                root(s + 2)
-            if done >= 0 and GROUP_TILES[done] > DMA_TILES:
-                add_bias_and_store(done, DMA_TILES, DMA_TILES)
 
         before_last, last = GROUPS - 2, GROUPS - 1
-        quantise(before_last, 0)
-        quantise(before_last, 1)
         project(before_last, range(PASSES))
-        quantise(last, 0)
         project(last, range(0, 1))
         add_bias_and_store(before_last, 0, DMA_TILES)
         quantise(last, 1)

@@ -33,7 +33,7 @@ GROUP_TILES = (2, 2, 4, 4, 4, 4, 4, 4, 2, 2)
 GROUPS = len(GROUP_TILES)
 MAX_TILES = max(GROUP_TILES)
 assert sum(GROUP_TILES) * P == ROWS
-VECTOR_TILES = (2, 1, 1, 1, 1, 1, 1, 1, 0, 0)
+VECTOR_TILES = (2, 0, 1, 1, 1, 1, 1, 1, 1, 0)
 LAG = 2
 DMA_TILES = 2
 PIECE_ROWS = 256
@@ -80,7 +80,10 @@ def tile_stulayer_pa_t_kernel(tc, src, ln1_w, ln1_b, w_uvqk_words, w_uvqk_scales
             for j in range(0, GROUP_TILES[u], tiles):
                 nc.sync.dma_start(out=x_tiles[u][:, j : j + tiles, :], in_=src_groups[u][:, j : j + tiles, :])
 
-        load(0, 1)
+        for j in range(GROUP_TILES[0]):
+            for c in range(BN_CHUNKS):
+                half = slice(c * BN_CHUNK, (c + 1) * BN_CHUNK)
+                nc.sync.dma_start(out=x_tiles[0][:, j, half], in_=src_groups[0][:, j, half])
         load(1, DMA_TILES)
         gain_bf = consts.tile([P, PASSES, PACK], BF16)
         shift_bf = consts.tile([P, PASSES, PACK], BF16)

@@ -33,7 +33,7 @@ GROUP_TILES = (2, 2, 4, 4, 4, 4, 4, 4, 2, 2)
 GROUPS = len(GROUP_TILES)
 MAX_TILES = max(GROUP_TILES)
 assert sum(GROUP_TILES) * P == ROWS
-VECTOR_TILES = (2, 0, 1, 1, 1, 1, 1, 1, 1, 0)
+VECTOR_TILES = (2, 0, 1, 1, 1, 1, 1, 1, 1, 1)
 LAG = 2
 DMA_TILES = 2
 PIECE_ROWS = 256
@@ -114,7 +114,7 @@ def tile_stulayer_pa_t_kernel(tc, src, ln1_w, ln1_b, w_uvqk_words, w_uvqk_scales
         eps = consts.tile([P, 1], F32)
         nc.vector.memset(eps[:], EPS)
         warm = consts.tile([P, 1], F32)
-        nc.scalar.activation(out=warm[:], in_=eps[:], func=ACT.Sqrt)
+        nc.scalar.activation(out=warm[:], in_=eps[:], func=ACT.Abs_reciprocal_sqrt)
         gain = consts.tile([P, PLANES], F32)
         shift = consts.tile([P, PLANES], F32)
         bias = consts.tile([P, N], F32)
@@ -143,23 +143,39 @@ def tile_stulayer_pa_t_kernel(tc, src, ln1_w, ln1_b, w_uvqk_words, w_uvqk_scales
                     out=chunk_stats[u][:, j, c, :], in_=x_tiles[u][:, j, c * BN_CHUNK : (c + 1) * BN_CHUNK]
                 )
 
-        def mean_and_variance(u):
-            mean_var = small.tile([P, MAX_TILES, BN_AGGR_DIM], F32, name="mean_var")
-            for j in range(GROUP_TILES[u]):
-                nc.vector.bn_aggr(out=mean_var[:, j, :], in_=chunk_stats[u][:, j].rearrange("p c v -> p (c v)"))
-            mean_vars[u] = mean_var
+        def mean_and_variance(u, tiles):
+            if u not in mean_vars:
+                mean_var = small.tile([P, MAX_TILES, BN_AGGR_DIM], F32, name="mean_var")
+                mean_vars[u] = mean_var
+            for j in tiles:
+                nc.vector.bn_aggr(out=mean_vars[u][:, j, :], in_=chunk_stats[u][:, j].rearrange("p c v -> p (c v)"))
+
+        def scalar_statistics(u, j):
+            if u not in mean_vars:
+                mean_var = small.tile([P, MAX_TILES, BN_AGGR_DIM], F32, name="mean_var")
+                mean_vars[u] = mean_var
+            unused = consts.tile([P, D], BF16, name="unused")
+            total = small.tile([P, 1], F32, name="total")
+            nc.scalar.activation(out=unused[:], in_=x_tiles[u][:, j, :], func=ACT.Identity, accum_out=total[:])
+            neg_mean = small.tile([P, 1], F32, name="neg_mean")
+            nc.scalar.activation(out=neg_mean[:], in_=total[:], func=ACT.Copy, scale=-1.0 / D)
+            squares = small.tile([P, 1], F32, name="squares")
+            nc.scalar.activation(
+                out=unused[:], in_=x_tiles[u][:, j, :], func=ACT.Square, bias=neg_mean[:], scale=1.0, accum_out=squares[:]
+            )
+            nc.scalar.activation(out=mean_vars[u][:, j, 0:1], in_=total[:], func=ACT.Copy, scale=1.0 / D)
+            nc.scalar.activation(out=mean_vars[u][:, j, 1:2], in_=squares[:], func=ACT.Copy, scale=1.0 / D)
 
         def root(u):
             n = GROUP_TILES[u]
-            std = small.tile([P, MAX_TILES], F32, name="std")
-            nc.scalar.activation(out=std[:, :n], in_=mean_vars[u][:, :n, 1], func=ACT.Sqrt, bias=eps[:], scale=1.0)
-            stds[u] = std
+            rstd = small.tile([P, MAX_TILES], F32, name="rstd")
+            nc.scalar.activation(
+                out=rstd[:, :n], in_=mean_vars[u][:, :n, 1], func=ACT.Abs_reciprocal_sqrt, bias=eps[:], scale=1.0
+            )
+            rstds[u] = rstd
 
         def invert_root(u):
-            n = GROUP_TILES[u]
-            rstd = small.tile([P, MAX_TILES], F32, name="rstd")
-            nc.vector.reciprocal(out=rstd[:, :n], in_=stds[u][:, :n])
-            rstds[u] = rstd
+            return
 
         def offset(u):
             n = GROUP_TILES[u]
@@ -179,14 +195,17 @@ def tile_stulayer_pa_t_kernel(tc, src, ln1_w, ln1_b, w_uvqk_words, w_uvqk_scales
                 sorted_out = xhat[:, j].rearrange("p (g t) q -> p g t q", t=PACK)
                 sorted_in = x_tiles[u][:, j, :].rearrange("p (g q t) -> p g t q", q=P, t=PACK)
                 if on_vector:
-                    nc.vector.tensor_scalar(
-                        out=sorted_out,
-                        in0=sorted_in,
-                        scalar1=mean_vars[u][:, j, 0:1],
-                        scalar2=rstds[u][:, j : j + 1],
-                        op0=ALU.subtract,
-                        op1=ALU.mult,
-                    )
+                    for g in range(PASSES):
+                        nc.vector.tensor_scalar(
+                            out=xhat[:, j, g * PACK : (g + 1) * PACK, :].rearrange("p t (c i) -> p c t i", i=4),
+                            in0=x_tiles[u][:, j, g * K_PASS : (g + 1) * K_PASS].rearrange(
+                                "p (c i t) -> p c t i", i=4, t=PACK
+                            ),
+                            scalar1=mean_vars[u][:, j, 0:1],
+                            scalar2=rstds[u][:, j : j + 1],
+                            op0=ALU.subtract,
+                            op1=ALU.mult,
+                        )
                 else:
                     for g in range(PASSES):
                         nc.scalar.activation(
@@ -281,16 +300,16 @@ def tile_stulayer_pa_t_kernel(tc, src, ln1_w, ln1_b, w_uvqk_words, w_uvqk_scales
             nc.sync.dma_start(out=out_groups[u][:, tiles, :], in_=out_sbs[u][:, tiles, :])
 
         chunk_statistics(0, range(half_rows(0)))
-        mean_and_variance(0)
+        mean_and_variance(0, range(GROUP_TILES[0]))
         root(0)
         nc.scalar.copy(out=gain[:], in_=gain_bf[:].rearrange("p g t -> p (g t)"))
         nc.scalar.copy(out=shift[:], in_=shift_bf[:].rearrange("p g t -> p (g t)"))
+        scalar_statistics(1, 1)
         chunk_statistics(1, range(0, 1))
         invert_root(0)
         chunk_statistics(1, range(1, 2))
         normalise(0, True)
-        chunk_statistics(1, range(2, half_rows(1)))
-        mean_and_variance(1)
+        mean_and_variance(1, range(0, 1))
         planes = transpose_and_scale(0, 0)
         regroup(0, 0, planes)
         root(1)
@@ -303,7 +322,7 @@ def tile_stulayer_pa_t_kernel(tc, src, ln1_w, ln1_b, w_uvqk_words, w_uvqk_scales
         planes = transpose_and_scale(0, 1)
         regroup(0, 1, planes)
         normalise(1, False)
-        mean_and_variance(2)
+        mean_and_variance(2, range(GROUP_TILES[2]))
         root(2)
         bias_sum = psum_acc.tile([P, N], F32, name="acc")
         nc.tensor.matmul(out=bias_sum[:], lhsT=ones[:], rhs=bias_row[:], start=True, stop=True)
@@ -319,7 +338,7 @@ def tile_stulayer_pa_t_kernel(tc, src, ln1_w, ln1_b, w_uvqk_words, w_uvqk_scales
             done = s - LAG
             if s + 2 < GROUPS:
                 chunk_statistics(s + 2, range(2 if s == 1 else 0, half_rows(s + 2)))
-                mean_and_variance(s + 2)
+                mean_and_variance(s + 2, range(GROUP_TILES[s + 2]))
             planes = transpose_and_scale(s, 0)
             regroup(s, 0, planes)
             if s + 1 < GROUPS:

from contextlib import ExitStack

import concourse.mybir as mybir
from concourse.masks import make_identity

FP8X4 = mybir.dt.float8_e4m3fn_x4
BF16 = mybir.dt.bfloat16
F32 = mybir.dt.float32
I32 = mybir.dt.int32
U32 = mybir.dt.uint32
U8 = mybir.dt.uint8
ALU = mybir.AluOpType
ACT = mybir.ActivationFunctionType

P = 128
PACK = 4
K_PASS = P * PACK
ROWS = 2048 * 2
D = 1024
N = 512
PASSES = D // K_PASS
PLANES = PASSES * PACK
BANK = 512
BN_CHUNK = 512
BN_CHUNKS = D // BN_CHUNK
BN_STATS_DIM = 6
BN_AGGR_DIM = 2
EPS = 1e-5

FLOPS = 2 * ROWS * D * N

GROUP_TILES = (2, 2, 4, 4, 4, 4, 4, 4, 2, 2)
GROUPS = len(GROUP_TILES)
MAX_TILES = max(GROUP_TILES)
assert sum(GROUP_TILES) * P == ROWS
VECTOR_TILES = (2, 0, 1, 1, 1, 1, 1, 1, 1, 1)
LAG = 2
DMA_TILES = 2
PIECE_ROWS = 256


def tile_stulayer_pa_t_kernel(tc, src, ln1_w, ln1_b, w_uvqk_words, w_uvqk_scales, b_uvqk, out):
    nc = tc.nc
    src_rows = src.rearrange("t b d -> (t b) d")
    out_rows = out.rearrange("t b n -> (t b) n")
    src_groups = []
    out_groups = []
    first_row = 0
    for n in GROUP_TILES:
        rows = slice(first_row, first_row + n * P)
        src_groups.append(src_rows[rows, :].rearrange("(p j) d -> p j d", j=n))
        out_groups.append(out_rows[rows, :].rearrange("(p j) n -> p j n", j=n))
        first_row += n * P

    with ExitStack() as ctx:
        consts = ctx.enter_context(tc.tile_pool(name="consts", bufs=1))
        x_pool = ctx.enter_context(tc.tile_pool(name="x", bufs=GROUPS))
        small = ctx.enter_context(tc.tile_pool(name="small", bufs=6))
        xhat_pool = ctx.enter_context(tc.tile_pool(name="xhat", bufs=3))
        plane_pool = ctx.enter_context(tc.tile_pool(name="planes", bufs=3))
        grouped_pool = ctx.enter_context(tc.tile_pool(name="grouped", bufs=PASSES * (LAG + 1)))
        mx_pool = ctx.enter_context(tc.tile_pool(name="mx", bufs=2))
        out_pool = ctx.enter_context(tc.tile_pool(name="outs", bufs=3))
        psum_t = ctx.enter_context(tc.psum_pool(name="psum_t", bufs=4))
        psum_acc = ctx.enter_context(tc.psum_pool(name="psum_acc", bufs=4))
        ctx.enter_context(tc.manual_schedule())

        w_scales = consts.tile([P, PASSES, N], U8, align_bytes=64)
        nc.vector.memset(w_scales[:].rearrange("p g n -> p (g n)").bitcast(I32), 0)
        bias_row = consts.tile([P, N], BF16)
        nc.vector.memset(bias_row[:], 0.0)
        ones = consts.tile([P, P], BF16)
        nc.vector.memset(ones[:], 1.0)
        x_tiles = []
        for u in range(GROUPS):
            x_sb = x_pool.tile([P, GROUP_TILES[u], D], BF16, name="x_sb")
            x_tiles.append(x_sb)

        def load(u, tiles):
            for j in range(0, GROUP_TILES[u], tiles):
                nc.sync.dma_start(out=x_tiles[u][:, j : j + tiles, :], in_=src_groups[u][:, j : j + tiles, :])

        for j in range(GROUP_TILES[0]):
            for c in range(BN_CHUNKS):
                half = slice(c * BN_CHUNK, (c + 1) * BN_CHUNK)
                nc.sync.dma_start(out=x_tiles[0][:, j, half], in_=src_groups[0][:, j, half])
        load(1, DMA_TILES)
        gain_bf = consts.tile([P, PASSES, PACK], BF16)
        shift_bf = consts.tile([P, PASSES, PACK], BF16)
        with nc.allow_non_contiguous_dma(reason="2 KiB vectors in runs of four features"):
            nc.sync.dma_start(out=gain_bf[:], in_=ln1_w.rearrange("(g p t) -> p g t", p=P, t=PACK))
            nc.sync.dma_start(out=shift_bf[:], in_=ln1_b.rearrange("(g p t) -> p g t", p=P, t=PACK))
        load(2, DMA_TILES)
        load(3, DMA_TILES)
        for g in range(PASSES):
            for quadrant in range(4):
                nc.sync.dma_start(
                    out=w_scales[32 * quadrant : 32 * quadrant + 4, g, :].bitcast(I32),
                    in_=w_uvqk_scales[g, 4 * quadrant : 4 * quadrant + 4, :].bitcast(I32),
                )
        w_words = consts.tile([P, PASSES, N], U32, align_bytes=64)
        for g in range(PASSES):
            nc.sync.dma_start(
                out=w_words[:, g, :].bitcast(I32),
                in_=w_uvqk_words[g].rearrange("p n t -> p (n t)").bitcast(I32),
            )
        for u in range(4, GROUPS):
            load(u, DMA_TILES)

        nc.scalar.dma_start(out=bias_row[0:1, :], in_=b_uvqk.rearrange("(o n) -> o n", o=1))

        identity = consts.tile([P, P], F32)
        make_identity(nc, identity[:])
        eps = consts.tile([P, 1], F32)
        nc.vector.memset(eps[:], EPS)
        warm = consts.tile([P, 1], F32)
        nc.scalar.activation(out=warm[:], in_=eps[:], func=ACT.Abs_reciprocal_sqrt)
        gain = consts.tile([P, PLANES], F32)
        shift = consts.tile([P, PLANES], F32)
        bias = consts.tile([P, N], F32)

        chunk_stats = {}
        mean_vars = {}
        stds = {}
        rstds = {}
        offsets = {}
        xhats = {}
        groupeds = {}
        operands = {}
        accs = {}
        out_sbs = {}

        def half_rows(u):
            return GROUP_TILES[u] * BN_CHUNKS

        def chunk_statistics(u, halves):
            if u not in chunk_stats:
                stats = small.tile([P, MAX_TILES, BN_CHUNKS, BN_STATS_DIM], F32, name="stats")
                chunk_stats[u] = stats
            for i in halves:
                j, c = divmod(i, BN_CHUNKS)
                nc.vector.bn_stats(
                    out=chunk_stats[u][:, j, c, :], in_=x_tiles[u][:, j, c * BN_CHUNK : (c + 1) * BN_CHUNK]
                )

        def mean_and_variance(u, tiles):
            if u not in mean_vars:
                mean_var = small.tile([P, MAX_TILES, BN_AGGR_DIM], F32, name="mean_var")
                mean_vars[u] = mean_var
            for j in tiles:
                nc.vector.bn_aggr(out=mean_vars[u][:, j, :], in_=chunk_stats[u][:, j].rearrange("p c v -> p (c v)"))

        def scalar_statistics(u, j):
            if u not in mean_vars:
                mean_var = small.tile([P, MAX_TILES, BN_AGGR_DIM], F32, name="mean_var")
                mean_vars[u] = mean_var
            unused = consts.tile([P, D], BF16, name="unused")
            total = small.tile([P, 1], F32, name="total")
            nc.scalar.activation(out=unused[:], in_=x_tiles[u][:, j, :], func=ACT.Identity, accum_out=total[:])
            neg_mean = small.tile([P, 1], F32, name="neg_mean")
            nc.scalar.activation(out=neg_mean[:], in_=total[:], func=ACT.Copy, scale=-1.0 / D)
            squares = small.tile([P, 1], F32, name="squares")
            nc.scalar.activation(
                out=unused[:], in_=x_tiles[u][:, j, :], func=ACT.Square, bias=neg_mean[:], scale=1.0, accum_out=squares[:]
            )
            nc.scalar.activation(out=mean_vars[u][:, j, 0:1], in_=total[:], func=ACT.Copy, scale=1.0 / D)
            nc.scalar.activation(out=mean_vars[u][:, j, 1:2], in_=squares[:], func=ACT.Copy, scale=1.0 / D)

        def root(u):
            n = GROUP_TILES[u]
            rstd = small.tile([P, MAX_TILES], F32, name="rstd")
            nc.scalar.activation(
                out=rstd[:, :n], in_=mean_vars[u][:, :n, 1], func=ACT.Abs_reciprocal_sqrt, bias=eps[:], scale=1.0
            )
            rstds[u] = rstd

        def invert_root(u):
            return

        def offset(u):
            n = GROUP_TILES[u]
            off = small.tile([P, MAX_TILES], F32, name="off")
            nc.vector.scalar_tensor_tensor(
                out=off[:, :n], in0=mean_vars[u][:, :n, 0], scalar=-1.0, in1=rstds[u][:, :n], op0=ALU.mult, op1=ALU.mult
            )
            offsets[u] = off

        def normalise(u, on_vector):
            if u not in xhats:
                xhat = xhat_pool.tile([P, MAX_TILES, PLANES, P], F32, name="xhat")
                xhats[u] = xhat
            xhat = xhats[u]
            split = GROUP_TILES[u] - VECTOR_TILES[u]
            for j in range(split, GROUP_TILES[u]) if on_vector else range(split):
                sorted_out = xhat[:, j].rearrange("p (g t) q -> p g t q", t=PACK)
                sorted_in = x_tiles[u][:, j, :].rearrange("p (g q t) -> p g t q", q=P, t=PACK)
                if on_vector:
                    for g in range(PASSES):
                        nc.vector.tensor_scalar(
                            out=xhat[:, j, g * PACK : (g + 1) * PACK, :].rearrange("p t (c i) -> p c t i", i=4),
                            in0=x_tiles[u][:, j, g * K_PASS : (g + 1) * K_PASS].rearrange(
                                "p (c i t) -> p c t i", i=4, t=PACK
                            ),
                            scalar1=mean_vars[u][:, j, 0:1],
                            scalar2=rstds[u][:, j : j + 1],
                            op0=ALU.subtract,
                            op1=ALU.mult,
                        )
                else:
                    for g in range(PASSES):
                        nc.scalar.activation(
                            out=xhat[:, j, g * PACK : (g + 1) * PACK, :].rearrange("p t (c i) -> p c t i", i=4),
                            in_=x_tiles[u][:, j, g * K_PASS : (g + 1) * K_PASS].rearrange(
                                "p (c i t) -> p c t i", i=4, t=PACK
                            ),
                            func=ACT.Identity,
                            scale=rstds[u][:, j : j + 1],
                            bias=offsets[u][:, j : j + 1],
                        )

        def transpose_and_scale(u, g):
            n = GROUP_TILES[u]
            width = n * P
            planes = plane_pool.tile([P, PACK, MAX_TILES * P], BF16, name="planes")
            in_bank = BANK // width
            for t0 in range(0, PACK, in_bank):
                xt = psum_t.tile([P, BANK], F32, name="xt")
                for i in range(in_bank):
                    for j in range(n):
                        nc.tensor.transpose(
                            xt[:, i * width + j * P : i * width + (j + 1) * P],
                            xhats[u][:, j, g * PACK + t0 + i, :],
                            identity[:],
                        )
                for i in range(in_bank):
                    plane = g * PACK + t0 + i
                    nc.scalar.activation(
                        out=planes[:, t0 + i, :width],
                        in_=xt[:, i * width : (i + 1) * width],
                        func=ACT.Identity,
                        scale=gain[:, plane : plane + 1],
                        bias=shift[:, plane : plane + 1],
                    )
            return planes

        def regroup(u, g, planes):
            grouped = grouped_pool.tile([P, MAX_TILES * P, PACK], BF16, align_bytes=64, name="grouped")
            for r0 in range(0, GROUP_TILES[u] * P, PIECE_ROWS):
                piece = slice(r0, r0 + PIECE_ROWS)
                nc.gpsimd.tensor_scalar(
                    out=grouped[:, piece, :].rearrange("p (c i) t -> p c t i", i=4),
                    in0=planes[:, :, piece].rearrange("p t (c i) -> p c t i", i=4),
                    scalar1=1.0,
                    scalar2=0.0,
                    op0=ALU.mult,
                    op1=ALU.add,
                )
            groupeds[u, g] = grouped

        def quantise(u, g):
            width = GROUP_TILES[u] * P
            if u not in operands:
                codes = mx_pool.tile([P, PASSES, MAX_TILES * P], U32, align_bytes=64, name="codes")
                scales = mx_pool.tile([P, PASSES, MAX_TILES * P], U8, align_bytes=64, name="scales")
                operands[u] = (codes, scales)
            codes, scales = operands[u]
            nc.vector.quantize_mx(
                out=codes[:, g, :width].bitcast(FP8X4),
                scales=scales[:, g, :width],
                in_=groupeds[u, g][:, :width, :].rearrange("p r t -> p (r t)"),
            )

        def project(u, passes):
            codes, scales = operands[u]
            if u not in accs:
                accs[u] = []
                for j in range(GROUP_TILES[u]):
                    acc = psum_acc.tile([P, N], F32, name="acc")
                    accs[u].append(acc)
            for g in passes:
                for j in range(GROUP_TILES[u]):
                    columns = slice(j * P, (j + 1) * P)
                    nc.tensor.matmul_mx(
                        out=accs[u][j][:],
                        lhsT=codes[:, g, columns].bitcast(FP8X4),
                        lhsT_scale=scales[:, g, columns],
                        rhs=w_words[:, g, :].bitcast(FP8X4),
                        rhs_scale=w_scales[:, g, :],
                        start=(g == 0),
                        stop=(g == PASSES - 1),
                    )

        def add_bias_and_store(u, j0, count):
            if j0 == 0:
                out_sb = out_pool.tile([P, MAX_TILES, N], F32, name="out_sb")
                out_sbs[u] = out_sb
            tiles = slice(j0, j0 + count)
            for j in range(j0, j0 + count):
                nc.vector.tensor_tensor(out=out_sbs[u][:, j, :], in0=accs[u][j][:], in1=bias[:], op=ALU.add)
            nc.sync.dma_start(out=out_groups[u][:, tiles, :], in_=out_sbs[u][:, tiles, :])

        chunk_statistics(0, range(half_rows(0)))
        mean_and_variance(0, range(GROUP_TILES[0]))
        root(0)
        nc.scalar.copy(out=gain[:], in_=gain_bf[:].rearrange("p g t -> p (g t)"))
        nc.scalar.copy(out=shift[:], in_=shift_bf[:].rearrange("p g t -> p (g t)"))
        scalar_statistics(1, 1)
        chunk_statistics(1, range(0, 1))
        invert_root(0)
        chunk_statistics(1, range(1, 2))
        normalise(0, True)
        mean_and_variance(1, range(0, 1))
        planes = transpose_and_scale(0, 0)
        regroup(0, 0, planes)
        root(1)
        chunk_statistics(2, range(0, 2))
        invert_root(1)
        chunk_statistics(2, range(2, 3))
        offset(1)
        normalise(1, True)
        chunk_statistics(2, range(3, half_rows(2)))
        planes = transpose_and_scale(0, 1)
        regroup(0, 1, planes)
        normalise(1, False)
        mean_and_variance(2, range(GROUP_TILES[2]))
        root(2)
        bias_sum = psum_acc.tile([P, N], F32, name="acc")
        nc.tensor.matmul(out=bias_sum[:], lhsT=ones[:], rhs=bias_row[:], start=True, stop=True)
        nc.scalar.copy(out=bias[:], in_=bias_sum[:])

        chunk_statistics(3, range(0, 2))
        invert_root(2)
        quantise(0, 0)
        offset(2)
        normalise(2, True)

        for s in range(1, GROUPS):
            done = s - LAG
            if s + 2 < GROUPS:
                chunk_statistics(s + 2, range(2 if s == 1 else 0, half_rows(s + 2)))
                mean_and_variance(s + 2, range(GROUP_TILES[s + 2]))
            planes = transpose_and_scale(s, 0)
            regroup(s, 0, planes)
            if s + 1 < GROUPS:
                normalise(s + 1, False)
            if s + 2 < GROUPS:
                root(s + 2)
            if done >= 0:
                project(done, range(PASSES))
                add_bias_and_store(done, 0, DMA_TILES)
                if GROUP_TILES[done] > DMA_TILES:
                    add_bias_and_store(done, DMA_TILES, DMA_TILES)
            quantise(s - 1, 1)
            if s + 2 < GROUPS:
                invert_root(s + 2)
            quantise(s, 0)
            if s + 2 < GROUPS:
                offset(s + 2)
                normalise(s + 2, True)
            planes = transpose_and_scale(s, 1)
            regroup(s, 1, planes)

        before_last, last = GROUPS - 2, GROUPS - 1
        project(before_last, range(PASSES))
        project(last, range(0, 1))
        add_bias_and_store(before_last, 0, DMA_TILES)
        quantise(last, 1)
        project(last, range(1, PASSES))
        for j in range(GROUP_TILES[last]):
            add_bias_and_store(last, j, 1)
